import numpy as np
import ml_dtypes


def mxq(x, axis, fmt="e4m3"):
    dtype, down = {"e4m3": (ml_dtypes.float8_e4m3fn, 7), "e5m2": (ml_dtypes.float8_e5m2, 14)}[fmt]
    v = np.moveaxis(np.asarray(x, np.float32).astype(ml_dtypes.bfloat16).astype(np.float64), axis, -1)
    blocks = v.reshape(v.shape[:-1] + (-1, 32))
    amax = np.abs(blocks).max(-1, keepdims=True)
    byte = np.maximum(np.where(amax > 0, np.frexp(amax)[1] - 1 + 127, 0) - down, 1)
    scale = np.exp2(byte - 127.0)
    codes = (blocks / scale).astype(np.float32).astype(dtype).astype(np.float64)
    return np.moveaxis((codes * scale).reshape(v.shape), -1, axis)


WIDE = False


def mx_kscale(k):
    if not WIDE:
        return np.ones(k)
    levels = np.array([10, -10, 5, -5, 0])
    a = np.random.permutation(np.resize(levels, k // 512 * 4)).reshape(k // 512, 4)
    idx = np.arange(k)
    return np.exp2(a[idx // 512, idx % 128 // 32])


BF16 = ml_dtypes.bfloat16


def bf(x):
    return np.asarray(x, np.float32).astype(BF16)


def f64(x):
    return np.asarray(x).astype(np.float64)


E2M1 = np.array([0.0, 0.5, 1.0, 1.5, 2.0, 3.0, 4.0, 6.0, -0.0, -0.5, -1.0, -1.5, -2.0, -3.0, -4.0, -6.0])


def pack_weight(w, fmt):
    k, n = w.shape
    w = f64(bf(w)).reshape(k // 32, 32, n)
    amax = np.abs(w).max(1)
    if fmt == "e4m3":
        byte = np.frexp(amax)[1] - 1 + 127 - 7
    else:
        mant, ex = np.frexp(amax / 6.0)
        byte = np.where(mant > 0.5, ex, ex - 1) + 127
    byte = np.clip(np.where(amax > 0, byte, 1), 1, 254)
    scaled = (w * np.exp2(127.0 - byte)[:, None, :]).reshape(k, n).astype(np.float32)
    by_word = np.ascontiguousarray(scaled.reshape(k // 512, 128, 4, n).transpose(0, 1, 3, 2))
    if fmt == "e4m3":
        words = by_word.astype(ml_dtypes.float8_e4m3fn).view(np.uint8)
    else:
        c = by_word.astype(ml_dtypes.float4_e2m1fn).view(np.uint8) & 0xF
        words = c[..., 0::2] | (c[..., 1::2] << 4)
    return np.ascontiguousarray(words), np.ascontiguousarray(byte.astype(np.uint8).reshape(k // 512, 16, n))


def unpack_weight(words, scales, fmt):
    g, p, n, _ = words.shape
    if fmt == "e4m3":
        vals = np.ascontiguousarray(words).view(ml_dtypes.float8_e4m3fn).astype(np.float64)
    else:
        nib = np.empty((g, p, n, 4), np.uint8)
        nib[..., 0::2] = words & 0xF
        nib[..., 1::2] = words >> 4
        vals = E2M1[nib]
    vals = vals * np.repeat(np.exp2(scales.astype(np.float64) - 127.0), 8, axis=1)[..., None]
    return vals.transpose(0, 1, 3, 2).reshape(g * 512, n)


B, TW, C, MS, RED = 8, 1024, 128, 4, 1
T = TW * MS
D = C * MS
F = D * RED


def sigmoid(v):
    return 1.0 / (1.0 + np.exp(-v))


def setup_inputs():
    t = mx_kscale(F)
    x = bf(np.random.standard_normal((B, T, C)))
    w1_words, w1_scales = pack_weight(np.random.standard_normal((D, F)) / np.sqrt(D) * t, "e4m3")
    w2_words, w2_scales = pack_weight(np.random.standard_normal((F, D)) * 3.0 / np.sqrt(F) / t[:, None], "e4m3")
    return {"x": x,
            "w1_words": w1_words, "w1_scales": w1_scales,
            "w2_words": w2_words, "w2_scales": w2_scales}


def reference(x, w1_words, w1_scales, w2_words, w2_scales):
    xt = f64(x).reshape(B, TW, MS, C).swapaxes(-1, -2)
    flat = xt.reshape(B, TW, D)
    h = np.maximum(mxq(flat, 2, "e4m3") @ unpack_weight(w1_words, w1_scales, "e4m3"), 0.0)
    a = mxq(h, 2, "e4m3") @ unpack_weight(w2_words, w2_scales, "e4m3")
    g = sigmoid(a).reshape(B, TW, C, MS)
    e = np.exp(g - g.max(-1, keepdims=True))
    y = e / e.sum(-1, keepdims=True)
    return (xt * y).sum(-1)

@@ -1,0 +1,280 @@
+from contextlib import ExitStack
+
+import concourse.mybir as mybir
+from concourse.masks import make_identity
+
+BF16 = mybir.dt.bfloat16
+F32 = mybir.dt.float32
+I32 = mybir.dt.int32
+U32 = mybir.dt.uint32
+U8 = mybir.dt.uint8
+FP8X4 = mybir.dt.float8_e4m3fn_x4
+ACT = mybir.ActivationFunctionType
+ALU = mybir.AluOpType
+
+P = 128
+MS = 4
+D = P * MS
+WINDOWS_IN_ALL = 8 * 1024
+TILES = 4
+WINDOWS = TILES * P
+BLOCKS = WINDOWS * MS // P
+ROUNDS = WINDOWS_IN_ALL // WINDOWS
+BANK_BF16 = 1024
+BANK_F32 = 512
+NORM_ROUNDS = 4
+
+FLOPS = 2 * 2 * WINDOWS_IN_ALL * D * D
+
+
+def tile_dwamformer_pa_t_kernel(tc, x, w1_words, w1_scales, w2_words, w2_scales, out):
+    nc = tc.nc
+    frames = x.flatten_outer_dims()
+    frames_by_round = frames.rearrange("(r b p) c -> r p b c", b=BLOCKS, p=P)
+    windows_by_round = frames.rearrange("(r t w m) c -> r w t (m c)", t=TILES, w=P, m=MS)
+    out_by_norm = out.flatten_outer_dims().rearrange(
+        "(n t w) c -> n w t c", t=NORM_ROUNDS * TILES, w=P
+    )
+
+    with ExitStack() as stack:
+        const = stack.enter_context(tc.tile_pool(name="const", bufs=1))
+        loads = stack.enter_context(tc.tile_pool(name="loads", bufs=4))
+        work = stack.enter_context(tc.tile_pool(name="work", bufs=2))
+        norm = stack.enter_context(tc.tile_pool(name="norm", bufs=2))
+        psum = stack.enter_context(tc.psum_pool(name="psum", bufs=2))
+        stack.enter_context(tc.manual_schedule())
+
+        x_by_frame = {}
+        x_by_window = {}
+        flat_grouped = {}
+        flat_mx = {}
+        hidden = {}
+        hidden_grouped = {}
+        hidden_mx = {}
+        squashed = {}
+        weights_and_products = {}
+        pair_sums = {}
+        totals = {}
+        log_of_sum = {}
+        inverse_of_sum = {}
+
+        def load_weight(words, scales, label):
+            codes = const.tile([P, D], U32, name=label + "_codes", align_bytes=64)
+            nc.sync.dma_start(
+                out=codes[:].bitcast(I32),
+                in_=words.rearrange("g p n t -> (g p) (n t)").bitcast(I32),
+            )
+            plane = const.tile([P, D], U8, name=label + "_plane", align_bytes=64)
+            nc.vector.memset(plane[:].bitcast(I32), 0)
+            rows = scales.rearrange("g q n -> (g q) n").bitcast(I32)
+            for quadrant in range(4):
+                nc.sync.dma_start(
+                    out=plane[32 * quadrant : 32 * quadrant + 4, :].bitcast(I32),
+                    in_=rows[4 * quadrant : 4 * quadrant + 4, :],
+                )
+            return codes, plane
+
+        def load_frames(r):
+            by_frame = loads.tile([P, BLOCKS, P], BF16)
+            nc.sync.dma_start(out=by_frame[:], in_=frames_by_round[r])
+            x_by_frame[r] = by_frame
+
+        def load_windows(r):
+            by_window = loads.tile([P, TILES, D], BF16)
+            nc.sync.dma_start(out=by_window[:], in_=windows_by_round[r])
+            x_by_window[r] = by_window
+
+        def quantise(grouped, label):
+            codes = work.tile([P, WINDOWS], U32, name=label + "_codes", align_bytes=64)
+            scales = work.tile([P, WINDOWS], U8, name=label + "_scales", align_bytes=64)
+            nc.vector.quantize_mx(out=codes[:].bitcast(FP8X4), scales=scales[:], in_=grouped[:])
+            return codes, scales
+
+        def turn_frames(r):
+            grouped = work.tile([P, WINDOWS * MS], BF16, name="flat_grouped", align_bytes=64)
+            blocks_in_bank = BANK_BF16 // P
+            for bank in range(BLOCKS // blocks_in_bank):
+                turned = psum.tile([P, BANK_BF16], BF16, name="frames_turned")
+                for b in range(blocks_in_bank):
+                    nc.tensor.transpose(
+                        turned[:, b * P : (b + 1) * P],
+                        x_by_frame[r][:, bank * blocks_in_bank + b, :],
+                        identity_bf16[:],
+                    )
+                dst = grouped[:, bank * BANK_BF16 : (bank + 1) * BANK_BF16]
+                if bank % 2 == 0:
+                    nc.scalar.copy(out=dst, in_=turned[:])
+                else:
+                    nc.vector.tensor_copy(out=dst, in_=turned[:])
+            flat_grouped[r] = grouped
+
+        def first_matmul(r):
+            codes, scales = flat_mx[r]
+            relu = work.tile([P, TILES, D], BF16, name="hidden")
+            for t in range(TILES):
+                cols = slice(t * P, (t + 1) * P)
+                acc = psum.tile([P, D], F32, name="hidden_acc")
+                nc.tensor.matmul_mx(
+                    out=acc[:],
+                    lhsT=codes[:, cols].bitcast(FP8X4),
+                    lhsT_scale=scales[:, cols],
+                    rhs=w1_codes[:].bitcast(FP8X4),
+                    rhs_scale=w1_plane[:],
+                    start=True,
+                    stop=True,
+                )
+                nc.scalar.activation(
+                    out=relu[:, t, :].rearrange("w (u p e) -> w u p e", u=2, e=2),
+                    in_=acc[:].rearrange("w (p u e) -> w u p e", u=2, e=2),
+                    func=ACT.Relu,
+                )
+            hidden[r] = relu
+
+        def turn_hidden(r):
+            words = hidden[r][:].bitcast(F32)
+            grouped = work.tile([P, WINDOWS * MS], BF16, name="hidden_grouped", align_bytes=64)
+            grouped_words = grouped[:].bitcast(F32)
+            tiles_in_bank = BANK_F32 // (2 * P)
+            for bank in range(TILES // tiles_in_bank):
+                turned = psum.tile([P, tiles_in_bank, 2, P], F32, name="hidden_turned")
+                for t in range(tiles_in_bank):
+                    for u in range(2):
+                        nc.tensor.transpose(
+                            turned[:, t, u, :],
+                            words[:, bank * tiles_in_bank + t, u * P : (u + 1) * P],
+                            identity_f32[:],
+                        )
+                dst = grouped_words[:, bank * BANK_F32 : (bank + 1) * BANK_F32].rearrange(
+                    "p (t w u) -> p t w u", t=tiles_in_bank, u=2
+                )
+                src = turned[:].rearrange("p t u w -> p t w u")
+                nc.vector.tensor_copy(out=dst, in_=src)
+            hidden_grouped[r] = grouped
+
+        def second_matmul(r):
+            codes, scales = hidden_mx[r]
+            tanh = work.tile([P, TILES, MS, P], F32, name="squashed")
+            for t in range(TILES):
+                cols = slice(t * P, (t + 1) * P)
+                acc = psum.tile([P, D], F32, name="gate_acc")
+                nc.tensor.matmul_mx(
+                    out=acc[:],
+                    lhsT=codes[:, cols].bitcast(FP8X4),
+                    lhsT_scale=scales[:, cols],
+                    rhs=w2_codes[:].bitcast(FP8X4),
+                    rhs_scale=w2_plane[:],
+                    start=True,
+                    stop=True,
+                )
+                nc.scalar.activation(
+                    out=tanh[:, t],
+                    in_=acc[:].rearrange("w (c m) -> w m c", m=MS),
+                    func=ACT.Tanh,
+                    scale=0.5,
+                )
+            squashed[r] = tanh
+
+        def exponentials(r):
+            both = work.tile([P, 2, TILES, MS, P], F32, name="weights_and_products")
+            for half in (slice(0, TILES // 2), slice(TILES // 2, TILES)):
+                nc.scalar.activation(
+                    out=both[:, 0, half], in_=squashed[r][:, half], func=ACT.Exp, scale=0.5
+                )
+            weights_and_products[r] = both
+
+        def products(r):
+            both = weights_and_products[r]
+            nc.vector.tensor_tensor(
+                out=both[:, 1].rearrange("w t m c -> w t (m c)"),
+                in0=both[:, 0].rearrange("w t m c -> w t (m c)"),
+                in1=x_by_window[r][:],
+                op=ALU.mult,
+            )
+
+        def sum_pairs(r):
+            both = weights_and_products[r][:].rearrange("w k t m c -> w (k t) m c")
+            pairs = work.tile([P, 2 * TILES, 2, P], F32, name="pair_sums")
+            nc.vector.tensor_tensor(
+                out=pairs[:], in0=both[:, :, 0:2, :], in1=both[:, :, 2:4, :], op=ALU.add
+            )
+            pair_sums[r] = pairs
+
+        def sum_all(r):
+            if r % NORM_ROUNDS == 0:
+                fresh = norm.tile([P, 2, NORM_ROUNDS, WINDOWS], F32, name="totals")
+                totals[r // NORM_ROUNDS] = fresh
+            pairs = pair_sums[r]
+            nc.vector.tensor_tensor(
+                out=totals[r // NORM_ROUNDS][:, :, r % NORM_ROUNDS, :].rearrange(
+                    "w k (t c) -> w k t c", t=TILES
+                ),
+                in0=pairs[:, :, 0, :].rearrange("w (k t) c -> w k t c", k=2),
+                in1=pairs[:, :, 1, :].rearrange("w (k t) c -> w k t c", k=2),
+                op=ALU.add,
+            )
+
+        def logarithms(n):
+            logs = norm.tile([P, NORM_ROUNDS, WINDOWS], F32, name="log_of_sum", bufs=1)
+            nc.scalar.activation(out=logs[:], in_=totals[n][:, 0], func=ACT.Ln)
+            log_of_sum[n] = logs
+
+        def inverses(n):
+            inverse = norm.tile([P, NORM_ROUNDS, WINDOWS], F32, name="inverse_of_sum", bufs=1)
+            nc.scalar.activation(out=inverse[:], in_=log_of_sum[n][:], func=ACT.Exp, scale=-1.0)
+            inverse_of_sum[n] = inverse
+
+        def divide_and_store(n):
+            pooled = norm.tile([P, NORM_ROUNDS, WINDOWS], F32, name="pooled")
+            nc.vector.tensor_tensor(
+                out=pooled[:], in0=totals[n][:, 1], in1=inverse_of_sum[n][:], op=ALU.mult
+            )
+            nc.gpsimd.dma_start(
+                out=out_by_norm[n], in_=pooled[:].rearrange("w r (t c) -> w (r t) c", t=TILES)
+            )
+
+        identity_bf16 = const.tile([P, P], BF16)
+        make_identity(nc, identity_bf16[:])
+        identity_f32 = const.tile([P, P], F32)
+        make_identity(nc, identity_f32[:])
+
+        load_frames(0)
+        w1_codes, w1_plane = load_weight(w1_words, w1_scales, "w1")
+        load_frames(1)
+        w2_codes, w2_plane = load_weight(w2_words, w2_scales, "w2")
+
+        def live(r):
+            return 0 <= r < ROUNDS
+
+        def closes_a_division(r):
+            return live(r) and r % NORM_ROUNDS == NORM_ROUNDS - 1
+
+        for step in range(ROUNDS + 4):
+            if live(step + 2):
+                load_frames(step + 2)
+            if live(step - 2):
+                hidden_mx[step - 2] = quantise(hidden_grouped[step - 2], "hidden")
+            if live(step):
+                load_windows(step)
+                turn_frames(step)
+            if live(step - 1):
+                first_matmul(step - 1)
+            if closes_a_division(step - 4):
+                inverses((step - 4) // NORM_ROUNDS)
+            if live(step - 2):
+                second_matmul(step - 2)
+            if live(step - 3):
+                products(step - 3)
+            if live(step):
+                flat_mx[step] = quantise(flat_grouped[step], "flat")
+            if live(step - 3):
+                sum_pairs(step - 3)
+            if live(step - 1):
+                turn_hidden(step - 1)
+            if live(step - 2):
+                exponentials(step - 2)
+            if live(step - 3):
+                sum_all(step - 3)
+            if closes_a_division(step - 3):
+                logarithms((step - 3) // NORM_ROUNDS)
+            if closes_a_division(step - 4):
+                divide_and_store((step - 4) // NORM_ROUNDS)

@@ -22,7 +22,8 @@ BLOCKS = WINDOWS * MS // P
 ROUNDS = WINDOWS_IN_ALL // WINDOWS
 BANK_BF16 = 1024
 BANK_F32 = 512
-NORM_ROUNDS = 4
+NORM_ROUNDS = 8
+PSUM_BANKS = 8
 
 FLOPS = 2 * 2 * WINDOWS_IN_ALL * D * D
 
@@ -32,17 +33,14 @@ def tile_dwamformer_pa_t_kernel(tc, x, w1_words, w1_scales, w2_words, w2_scales,
     frames = x.flatten_outer_dims()
     frames_by_round = frames.rearrange("(r b p) c -> r p b c", b=BLOCKS, p=P)
     windows_by_round = frames.rearrange("(r t w m) c -> r w t (m c)", t=TILES, w=P, m=MS)
-    out_by_norm = out.flatten_outer_dims().rearrange(
-        "(n t w) c -> n w t c", t=NORM_ROUNDS * TILES, w=P
-    )
+    out_by_round = out.flatten_outer_dims().rearrange("(r t w) c -> r w t c", t=TILES, w=P)
 
     with ExitStack() as stack:
         const = stack.enter_context(tc.tile_pool(name="const", bufs=1))
         loads = stack.enter_context(tc.tile_pool(name="loads", bufs=4))
-        work = stack.enter_context(tc.tile_pool(name="work", bufs=2))
+        work = stack.enter_context(tc.tile_pool(name="work", bufs=3))
         norm = stack.enter_context(tc.tile_pool(name="norm", bufs=2))
-        psum = stack.enter_context(tc.psum_pool(name="psum", bufs=2))
-        stack.enter_context(tc.manual_schedule())
+        psum = stack.enter_context(tc.psum_pool(name="psum", bufs=PSUM_BANKS))
 
         x_by_frame = {}
         x_by_window = {}
@@ -51,12 +49,9 @@ def tile_dwamformer_pa_t_kernel(tc, x, w1_words, w1_scales, w2_words, w2_scales,
         hidden = {}
         hidden_grouped = {}
         hidden_mx = {}
-        squashed = {}
         weights_and_products = {}
         pair_sums = {}
         totals = {}
-        log_of_sum = {}
-        inverse_of_sum = {}
 
         def load_weight(words, scales, label):
             codes = const.tile([P, D], U32, name=label + "_codes", align_bytes=64)
@@ -94,7 +89,7 @@ def tile_dwamformer_pa_t_kernel(tc, x, w1_words, w1_scales, w2_words, w2_scales,
             grouped = work.tile([P, WINDOWS * MS], BF16, name="flat_grouped", align_bytes=64)
             blocks_in_bank = BANK_BF16 // P
             for bank in range(BLOCKS // blocks_in_bank):
-                turned = psum.tile([P, BANK_BF16], BF16, name="frames_turned")
+                turned = psum.tile([P, BANK_BF16], BF16, name="frames_turned", tag="bank")
                 for b in range(blocks_in_bank):
                     nc.tensor.transpose(
                         turned[:, b * P : (b + 1) * P],
@@ -113,7 +108,7 @@ def tile_dwamformer_pa_t_kernel(tc, x, w1_words, w1_scales, w2_words, w2_scales,
             relu = work.tile([P, TILES, D], BF16, name="hidden")
             for t in range(TILES):
                 cols = slice(t * P, (t + 1) * P)
-                acc = psum.tile([P, D], F32, name="hidden_acc")
+                acc = psum.tile([P, D], F32, name="hidden_acc", tag="bank")
                 nc.tensor.matmul_mx(
                     out=acc[:],
                     lhsT=codes[:, cols].bitcast(FP8X4),
@@ -123,11 +118,12 @@ def tile_dwamformer_pa_t_kernel(tc, x, w1_words, w1_scales, w2_words, w2_scales,
                     start=True,
                     stop=True,
                 )
-                nc.scalar.activation(
-                    out=relu[:, t, :].rearrange("w (u p e) -> w u p e", u=2, e=2),
-                    in_=acc[:].rearrange("w (p u e) -> w u p e", u=2, e=2),
-                    func=ACT.Relu,
-                )
+                dst = relu[:, t, :].rearrange("w (u p e) -> w u p e", u=2, e=2)
+                src = acc[:].rearrange("w (p u e) -> w u p e", u=2, e=2)
+                if t == 0:
+                    nc.vector.tensor_relu(out=dst, in_=src)
+                else:
+                    nc.scalar.activation(out=dst, in_=src, func=ACT.Relu)
             hidden[r] = relu
 
         def turn_hidden(r):
@@ -136,7 +132,7 @@ def tile_dwamformer_pa_t_kernel(tc, x, w1_words, w1_scales, w2_words, w2_scales,
             grouped_words = grouped[:].bitcast(F32)
             tiles_in_bank = BANK_F32 // (2 * P)
             for bank in range(TILES // tiles_in_bank):
-                turned = psum.tile([P, tiles_in_bank, 2, P], F32, name="hidden_turned")
+                turned = psum.tile([P, tiles_in_bank, 2, P], F32, name="hidden_turned", tag="bank")
                 for t in range(tiles_in_bank):
                     for u in range(2):
                         nc.tensor.transpose(
@@ -153,10 +149,10 @@ def tile_dwamformer_pa_t_kernel(tc, x, w1_words, w1_scales, w2_words, w2_scales,
 
         def second_matmul(r):
             codes, scales = hidden_mx[r]
-            tanh = work.tile([P, TILES, MS, P], F32, name="squashed")
+            both = work.tile([P, 2, TILES, MS, P], F32, name="weights_and_products")
             for t in range(TILES):
                 cols = slice(t * P, (t + 1) * P)
-                acc = psum.tile([P, D], F32, name="gate_acc")
+                acc = psum.tile([P, D], F32, name="gate_acc", tag="bank")
                 nc.tensor.matmul_mx(
                     out=acc[:],
                     lhsT=codes[:, cols].bitcast(FP8X4),
@@ -167,20 +163,19 @@ def tile_dwamformer_pa_t_kernel(tc, x, w1_words, w1_scales, w2_words, w2_scales,
                     stop=True,
                 )
                 nc.scalar.activation(
-                    out=tanh[:, t],
+                    out=both[:, 0, t],
                     in_=acc[:].rearrange("w (c m) -> w m c", m=MS),
                     func=ACT.Tanh,
                     scale=0.5,
                 )
-            squashed[r] = tanh
+            weights_and_products[r] = both
 
         def exponentials(r):
-            both = work.tile([P, 2, TILES, MS, P], F32, name="weights_and_products")
+            both = weights_and_products[r]
             for half in (slice(0, TILES // 2), slice(TILES // 2, TILES)):
                 nc.scalar.activation(
-                    out=both[:, 0, half], in_=squashed[r][:, half], func=ACT.Exp, scale=0.5
+                    out=both[:, 0, half], in_=both[:, 0, half], func=ACT.Exp, scale=0.5
                 )
-            weights_and_products[r] = both
 
         def products(r):
             both = weights_and_products[r]
@@ -193,19 +188,34 @@ def tile_dwamformer_pa_t_kernel(tc, x, w1_words, w1_scales, w2_words, w2_scales,
 
         def sum_pairs(r):
             both = weights_and_products[r][:].rearrange("w k t m c -> w (k t) m c")
-            pairs = work.tile([P, 2 * TILES, 2, P], F32, name="pair_sums")
+            pairs = work.tile([P, 2 * TILES, 2, P], F32, name="pair_sums", bufs=2)
             nc.vector.tensor_tensor(
                 out=pairs[:], in0=both[:, :, 0:2, :], in1=both[:, :, 2:4, :], op=ALU.add
             )
             pair_sums[r] = pairs
 
+        def live(r):
+            return 0 <= r < ROUNDS
+
+        def division_of(r):
+            return (r + 1) // NORM_ROUNDS
+
+        def place_of(r):
+            return (r + 1) % NORM_ROUNDS
+
+        def closes_a_division(r):
+            return live(r) and (r == ROUNDS - 1 or division_of(r + 1) != division_of(r))
+
+        def rounds_of(n):
+            return [r for r in range(ROUNDS) if division_of(r) == n]
+
         def sum_all(r):
-            if r % NORM_ROUNDS == 0:
+            if r == rounds_of(division_of(r))[0]:
                 fresh = norm.tile([P, 2, NORM_ROUNDS, WINDOWS], F32, name="totals")
-                totals[r // NORM_ROUNDS] = fresh
+                totals[division_of(r)] = fresh
             pairs = pair_sums[r]
-            nc.vector.tensor_tensor(
-                out=totals[r // NORM_ROUNDS][:, :, r % NORM_ROUNDS, :].rearrange(
+            nc.gpsimd.tensor_tensor(
+                out=totals[division_of(r)][:, :, place_of(r), :].rearrange(
                     "w k (t c) -> w k t c", t=TILES
                 ),
                 in0=pairs[:, :, 0, :].rearrange("w (k t) c -> w k t c", k=2),
@@ -214,23 +224,21 @@ def tile_dwamformer_pa_t_kernel(tc, x, w1_words, w1_scales, w2_words, w2_scales,
             )
 
         def logarithms(n):
-            logs = norm.tile([P, NORM_ROUNDS, WINDOWS], F32, name="log_of_sum", bufs=1)
-            nc.scalar.activation(out=logs[:], in_=totals[n][:, 0], func=ACT.Ln)
-            log_of_sum[n] = logs
-
-        def inverses(n):
-            inverse = norm.tile([P, NORM_ROUNDS, WINDOWS], F32, name="inverse_of_sum", bufs=1)
-            nc.scalar.activation(out=inverse[:], in_=log_of_sum[n][:], func=ACT.Exp, scale=-1.0)
-            inverse_of_sum[n] = inverse
+            places = slice(place_of(rounds_of(n)[0]), place_of(rounds_of(n)[-1]) + 1)
+            sums = totals[n][:, 0, places, :]
+            nc.scalar.activation(out=sums, in_=sums, func=ACT.Ln)
 
         def divide_and_store(n):
-            pooled = norm.tile([P, NORM_ROUNDS, WINDOWS], F32, name="pooled")
-            nc.vector.tensor_tensor(
-                out=pooled[:], in0=totals[n][:, 1], in1=inverse_of_sum[n][:], op=ALU.mult
-            )
-            nc.gpsimd.dma_start(
-                out=out_by_norm[n], in_=pooled[:].rearrange("w r (t c) -> w (r t) c", t=TILES)
-            )
+            for r in rounds_of(n):
+                log_of_sum = totals[n][:, 0, place_of(r), :]
+                nc.scalar.activation(out=log_of_sum, in_=log_of_sum, func=ACT.Exp, scale=-1.0)
+                pooled = norm.tile([P, WINDOWS], F32, name="pooled", bufs=3)
+                nc.gpsimd.tensor_tensor(
+                    out=pooled[:], in0=totals[n][:, 1, place_of(r), :], in1=log_of_sum, op=ALU.mult
+                )
+                nc.sync.dma_start(
+                    out=out_by_round[r], in_=pooled[:].rearrange("w (t c) -> w t c", t=TILES)
+                )
 
         identity_bf16 = const.tile([P, P], BF16)
         make_identity(nc, identity_bf16[:])
@@ -242,12 +250,6 @@ def tile_dwamformer_pa_t_kernel(tc, x, w1_words, w1_scales, w2_words, w2_scales,
         load_frames(1)
         w2_codes, w2_plane = load_weight(w2_words, w2_scales, "w2")
 
-        def live(r):
-            return 0 <= r < ROUNDS
-
-        def closes_a_division(r):
-            return live(r) and r % NORM_ROUNDS == NORM_ROUNDS - 1
-
         for step in range(ROUNDS + 4):
             if live(step + 2):
                 load_frames(step + 2)
@@ -258,8 +260,6 @@ def tile_dwamformer_pa_t_kernel(tc, x, w1_words, w1_scales, w2_words, w2_scales,
                 turn_frames(step)
             if live(step - 1):
                 first_matmul(step - 1)
-            if closes_a_division(step - 4):
-                inverses((step - 4) // NORM_ROUNDS)
             if live(step - 2):
                 second_matmul(step - 2)
             if live(step - 3):
@@ -275,6 +275,6 @@ def tile_dwamformer_pa_t_kernel(tc, x, w1_words, w1_scales, w2_words, w2_scales,
             if live(step - 3):
                 sum_all(step - 3)
             if closes_a_division(step - 3):
-                logarithms((step - 3) // NORM_ROUNDS)
+                logarithms(division_of(step - 3))
             if closes_a_division(step - 4):
-                divide_and_store((step - 4) // NORM_ROUNDS)
+                divide_and_store(division_of(step - 4))

@@ -118,12 +118,11 @@ def tile_dwamformer_pa_t_kernel(tc, x, w1_words, w1_scales, w2_words, w2_scales,
                     start=True,
                     stop=True,
                 )
-                dst = relu[:, t, :].rearrange("w (u p e) -> w u p e", u=2, e=2)
-                src = acc[:].rearrange("w (p u e) -> w u p e", u=2, e=2)
-                if t == 0:
-                    nc.vector.tensor_relu(out=dst, in_=src)
-                else:
-                    nc.scalar.activation(out=dst, in_=src, func=ACT.Relu)
+                nc.scalar.activation(
+                    out=relu[:, t, :].rearrange("w (u p e) -> w u p e", u=2, e=2),
+                    in_=acc[:].rearrange("w (p u e) -> w u p e", u=2, e=2),
+                    func=ACT.Relu,
+                )
             hidden[r] = relu
 
         def turn_hidden(r):
@@ -214,7 +213,7 @@ def tile_dwamformer_pa_t_kernel(tc, x, w1_words, w1_scales, w2_words, w2_scales,
                 fresh = norm.tile([P, 2, NORM_ROUNDS, WINDOWS], F32, name="totals")
                 totals[division_of(r)] = fresh
             pairs = pair_sums[r]
-            nc.gpsimd.tensor_tensor(
+            nc.vector.tensor_tensor(
                 out=totals[division_of(r)][:, :, place_of(r), :].rearrange(
                     "w k (t c) -> w k t c", t=TILES
                 ),
@@ -233,10 +232,10 @@ def tile_dwamformer_pa_t_kernel(tc, x, w1_words, w1_scales, w2_words, w2_scales,
                 log_of_sum = totals[n][:, 0, place_of(r), :]
                 nc.scalar.activation(out=log_of_sum, in_=log_of_sum, func=ACT.Exp, scale=-1.0)
                 pooled = norm.tile([P, WINDOWS], F32, name="pooled", bufs=3)
-                nc.gpsimd.tensor_tensor(
+                nc.vector.tensor_tensor(
                     out=pooled[:], in0=totals[n][:, 1, place_of(r), :], in1=log_of_sum, op=ALU.mult
                 )
-                nc.sync.dma_start(
+                nc.gpsimd.dma_start(
                     out=out_by_round[r], in_=pooled[:].rearrange("w (t c) -> w t c", t=TILES)
                 )
 

@@ -50,7 +50,6 @@ def tile_dwamformer_pa_t_kernel(tc, x, w1_words, w1_scales, w2_words, w2_scales,
         hidden_grouped = {}
         hidden_mx = {}
         weights_and_products = {}
-        pair_sums = {}
         totals = {}
 
         def load_weight(words, scales, label):
@@ -118,11 +117,12 @@ def tile_dwamformer_pa_t_kernel(tc, x, w1_words, w1_scales, w2_words, w2_scales,
                     start=True,
                     stop=True,
                 )
-                nc.scalar.activation(
-                    out=relu[:, t, :].rearrange("w (u p e) -> w u p e", u=2, e=2),
-                    in_=acc[:].rearrange("w (p u e) -> w u p e", u=2, e=2),
-                    func=ACT.Relu,
-                )
+                dst = relu[:, t, :].rearrange("w (u p e) -> w u p e", u=2, e=2)
+                src = acc[:].rearrange("w (p u e) -> w u p e", u=2, e=2)
+                if t == 0:
+                    nc.vector.tensor_relu(out=dst, in_=src)
+                else:
+                    nc.scalar.activation(out=dst, in_=src, func=ACT.Relu)
             hidden[r] = relu
 
         def turn_hidden(r):
@@ -148,7 +148,7 @@ def tile_dwamformer_pa_t_kernel(tc, x, w1_words, w1_scales, w2_words, w2_scales,
 
         def second_matmul(r):
             codes, scales = hidden_mx[r]
-            both = work.tile([P, 2, TILES, MS, P], F32, name="weights_and_products")
+            both = work.tile([P, 2, TILES, P, MS], F32, name="weights_and_products")
             for t in range(TILES):
                 cols = slice(t * P, (t + 1) * P)
                 acc = psum.tile([P, D], F32, name="gate_acc", tag="bank")
@@ -162,8 +162,8 @@ def tile_dwamformer_pa_t_kernel(tc, x, w1_words, w1_scales, w2_words, w2_scales,
                     stop=True,
                 )
                 nc.scalar.activation(
-                    out=both[:, 0, t],
-                    in_=acc[:].rearrange("w (c m) -> w m c", m=MS),
+                    out=both[:, 0, t].rearrange("w c m -> w (c m)"),
+                    in_=acc[:],
                     func=ACT.Tanh,
                     scale=0.5,
                 )
@@ -178,20 +178,12 @@ def tile_dwamformer_pa_t_kernel(tc, x, w1_words, w1_scales, w2_words, w2_scales,
 
         def products(r):
             both = weights_and_products[r]
-            nc.vector.tensor_tensor(
-                out=both[:, 1].rearrange("w t m c -> w t (m c)"),
-                in0=both[:, 0].rearrange("w t m c -> w t (m c)"),
-                in1=x_by_window[r][:],
+            nc.gpsimd.tensor_tensor(
+                out=both[:, 1],
+                in0=both[:, 0],
+                in1=x_by_window[r][:].rearrange("w t (m c) -> w t c m", m=MS),
                 op=ALU.mult,
             )
-
-        def sum_pairs(r):
-            both = weights_and_products[r][:].rearrange("w k t m c -> w (k t) m c")
-            pairs = work.tile([P, 2 * TILES, 2, P], F32, name="pair_sums", bufs=2)
-            nc.vector.tensor_tensor(
-                out=pairs[:], in0=both[:, :, 0:2, :], in1=both[:, :, 2:4, :], op=ALU.add
-            )
-            pair_sums[r] = pairs
 
         def live(r):
             return 0 <= r < ROUNDS
@@ -208,17 +200,14 @@ def tile_dwamformer_pa_t_kernel(tc, x, w1_words, w1_scales, w2_words, w2_scales,
         def rounds_of(n):
             return [r for r in range(ROUNDS) if division_of(r) == n]
 
-        def sum_all(r):
-            if r == rounds_of(division_of(r))[0]:
+        def sum_frames(r, kind):
+            if kind == 0 and r == rounds_of(division_of(r))[0]:
                 fresh = norm.tile([P, 2, NORM_ROUNDS, WINDOWS], F32, name="totals")
                 totals[division_of(r)] = fresh
-            pairs = pair_sums[r]
-            nc.vector.tensor_tensor(
-                out=totals[division_of(r)][:, :, place_of(r), :].rearrange(
-                    "w k (t c) -> w k t c", t=TILES
-                ),
-                in0=pairs[:, :, 0, :].rearrange("w (k t) c -> w k t c", k=2),
-                in1=pairs[:, :, 1, :].rearrange("w (k t) c -> w k t c", k=2),
+            nc.vector.tensor_reduce(
+                out=totals[division_of(r)][:, kind, place_of(r), :],
+                in_=weights_and_products[r][:, kind].rearrange("w t c m -> w (t c) m"),
+                axis=mybir.AxisListType.X,
                 op=ALU.add,
             )
 
@@ -232,10 +221,10 @@ def tile_dwamformer_pa_t_kernel(tc, x, w1_words, w1_scales, w2_words, w2_scales,
                 log_of_sum = totals[n][:, 0, place_of(r), :]
                 nc.scalar.activation(out=log_of_sum, in_=log_of_sum, func=ACT.Exp, scale=-1.0)
                 pooled = norm.tile([P, WINDOWS], F32, name="pooled", bufs=3)
-                nc.vector.tensor_tensor(
+                nc.gpsimd.tensor_tensor(
                     out=pooled[:], in0=totals[n][:, 1, place_of(r), :], in1=log_of_sum, op=ALU.mult
                 )
-                nc.gpsimd.dma_start(
+                nc.sync.dma_start(
                     out=out_by_round[r], in_=pooled[:].rearrange("w (t c) -> w t c", t=TILES)
                 )
 
@@ -266,13 +255,13 @@ def tile_dwamformer_pa_t_kernel(tc, x, w1_words, w1_scales, w2_words, w2_scales,
             if live(step):
                 flat_mx[step] = quantise(flat_grouped[step], "flat")
             if live(step - 3):
-                sum_pairs(step - 3)
+                sum_frames(step - 3, 0)
             if live(step - 1):
                 turn_hidden(step - 1)
             if live(step - 2):
                 exponentials(step - 2)
             if live(step - 3):
-                sum_all(step - 3)
+                sum_frames(step - 3, 1)
             if closes_a_division(step - 3):
                 logarithms(division_of(step - 3))
             if closes_a_division(step - 4):

@@ -22,7 +22,7 @@ BLOCKS = WINDOWS * MS // P
 ROUNDS = WINDOWS_IN_ALL // WINDOWS
 BANK_BF16 = 1024
 BANK_F32 = 512
-NORM_ROUNDS = 8
+NORM_ROUNDS = 6
 PSUM_BANKS = 8
 
 FLOPS = 2 * 2 * WINDOWS_IN_ALL * D * D
@@ -50,7 +50,8 @@ def tile_dwamformer_pa_t_kernel(tc, x, w1_words, w1_scales, w2_words, w2_scales,
         hidden_grouped = {}
         hidden_mx = {}
         weights_and_products = {}
-        totals = {}
+        sums_of_weights = {}
+        sums_of_products = {}
 
         def load_weight(words, scales, label):
             codes = const.tile([P, D], U32, name=label + "_codes", align_bytes=64)
@@ -148,7 +149,7 @@ def tile_dwamformer_pa_t_kernel(tc, x, w1_words, w1_scales, w2_words, w2_scales,
 
         def second_matmul(r):
             codes, scales = hidden_mx[r]
-            both = work.tile([P, 2, TILES, P, MS], F32, name="weights_and_products")
+            both = work.tile([P, 2, TILES, MS, P], F32, name="weights_and_products")
             for t in range(TILES):
                 cols = slice(t * P, (t + 1) * P)
                 acc = psum.tile([P, D], F32, name="gate_acc", tag="bank")
@@ -162,8 +163,8 @@ def tile_dwamformer_pa_t_kernel(tc, x, w1_words, w1_scales, w2_words, w2_scales,
                     stop=True,
                 )
                 nc.scalar.activation(
-                    out=both[:, 0, t].rearrange("w c m -> w (c m)"),
-                    in_=acc[:],
+                    out=both[:, 0, t],
+                    in_=acc[:].rearrange("w (c m) -> w m c", m=MS),
                     func=ACT.Tanh,
                     scale=0.5,
                 )
@@ -178,21 +179,60 @@ def tile_dwamformer_pa_t_kernel(tc, x, w1_words, w1_scales, w2_words, w2_scales,
 
         def products(r):
             both = weights_and_products[r]
-            nc.gpsimd.tensor_tensor(
-                out=both[:, 1],
-                in0=both[:, 0],
-                in1=x_by_window[r][:].rearrange("w t (m c) -> w t c m", m=MS),
+            nc.vector.tensor_tensor(
+                out=both[:, 1].rearrange("w t m c -> w t (m c)"),
+                in0=both[:, 0].rearrange("w t m c -> w t (m c)"),
+                in1=x_by_window[r][:],
                 op=ALU.mult,
+            )
+
+        def sum_weights(r):
+            if r == rounds_of(division_of(r))[0]:
+                fresh = norm.tile([P, NORM_ROUNDS, WINDOWS], F32, name="sums_of_weights")
+                sums_of_weights[division_of(r)] = fresh
+            both = weights_and_products[r]
+            turned = psum.tile([P, TILES, P], F32, name="weights_turned", tag="bank")
+            for t in range(TILES):
+                for m in range(MS):
+                    nc.tensor.matmul(
+                        out=turned[:, t, :],
+                        lhsT=both[:, 0, t, m, :],
+                        rhs=identity_f32[:],
+                        is_transpose=True,
+                        start=(m == 0),
+                        stop=(m == MS - 1),
+                    )
+            nc.vector.tensor_copy(
+                out=sums_of_weights[division_of(r)][:, place_of(r), :],
+                in_=turned[:].rearrange("c t w -> c (t w)"),
+            )
+
+        def sum_products(r):
+            if r == rounds_of(division_of(r))[0]:
+                fresh = norm.tile([P, NORM_ROUNDS, WINDOWS], F32, name="sums_of_products")
+                sums_of_products[division_of(r)] = fresh
+            both = weights_and_products[r]
+            pairs = work.tile([P, TILES, 2, P], F32, name="pair_sums", bufs=2)
+            nc.vector.tensor_tensor(
+                out=pairs[:], in0=both[:, 1, :, 0:2, :], in1=both[:, 1, :, 2:4, :], op=ALU.add
+            )
+            nc.vector.tensor_tensor(
+                out=sums_of_products[division_of(r)][:, place_of(r), :].rearrange(
+                    "w (t c) -> w t c", t=TILES
+                ),
+                in0=pairs[:, :, 0, :],
+                in1=pairs[:, :, 1, :],
+                op=ALU.add,
             )
 
         def live(r):
             return 0 <= r < ROUNDS
 
         def division_of(r):
-            return (r + 1) // NORM_ROUNDS
+            return r // NORM_ROUNDS
 
         def place_of(r):
-            return (r + 1) % NORM_ROUNDS
+            return r % NORM_ROUNDS
 
         def closes_a_division(r):
             return live(r) and (r == ROUNDS - 1 or division_of(r + 1) != division_of(r))
@@ -200,29 +240,26 @@ def tile_dwamformer_pa_t_kernel(tc, x, w1_words, w1_scales, w2_words, w2_scales,
         def rounds_of(n):
             return [r for r in range(ROUNDS) if division_of(r) == n]
 
-        def sum_frames(r, kind):
-            if kind == 0 and r == rounds_of(division_of(r))[0]:
-                fresh = norm.tile([P, 2, NORM_ROUNDS, WINDOWS], F32, name="totals")
-                totals[division_of(r)] = fresh
-            nc.vector.tensor_reduce(
-                out=totals[division_of(r)][:, kind, place_of(r), :],
-                in_=weights_and_products[r][:, kind].rearrange("w t c m -> w (t c) m"),
-                axis=mybir.AxisListType.X,
-                op=ALU.add,
-            )
-
         def logarithms(n):
             places = slice(place_of(rounds_of(n)[0]), place_of(rounds_of(n)[-1]) + 1)
-            sums = totals[n][:, 0, places, :]
+            sums = sums_of_weights[n][:, places, :]
             nc.scalar.activation(out=sums, in_=sums, func=ACT.Ln)
 
         def divide_and_store(n):
             for r in rounds_of(n):
-                log_of_sum = totals[n][:, 0, place_of(r), :]
-                nc.scalar.activation(out=log_of_sum, in_=log_of_sum, func=ACT.Exp, scale=-1.0)
+                cell = sums_of_weights[n][:, place_of(r), :]
+                nc.scalar.activation(out=cell, in_=cell, func=ACT.Exp, scale=-1.0)
+                inverse = psum.tile([P, TILES, P], F32, name="inverse", tag="bank")
+                for t in range(TILES):
+                    nc.tensor.transpose(
+                        inverse[:, t, :], cell[:, t * P : (t + 1) * P], identity_f32[:]
+                    )
                 pooled = norm.tile([P, WINDOWS], F32, name="pooled", bufs=3)
-                nc.gpsimd.tensor_tensor(
-                    out=pooled[:], in0=totals[n][:, 1, place_of(r), :], in1=log_of_sum, op=ALU.mult
+                nc.vector.tensor_tensor(
+                    out=pooled[:],
+                    in0=sums_of_products[n][:, place_of(r), :],
+                    in1=inverse[:].rearrange("w t c -> w (t c)"),
+                    op=ALU.mult,
                 )
                 nc.sync.dma_start(
                     out=out_by_round[r], in_=pooled[:].rearrange("w (t c) -> w t c", t=TILES)
@@ -246,22 +283,19 @@ def tile_dwamformer_pa_t_kernel(tc, x, w1_words, w1_scales, w2_words, w2_scales,
             if live(step):
                 load_windows(step)
                 turn_frames(step)
+                flat_mx[step] = quantise(flat_grouped[step], "flat")
             if live(step - 1):
                 first_matmul(step - 1)
             if live(step - 2):
                 second_matmul(step - 2)
-            if live(step - 3):
-                products(step - 3)
-            if live(step):
-                flat_mx[step] = quantise(flat_grouped[step], "flat")
-            if live(step - 3):
-                sum_frames(step - 3, 0)
             if live(step - 1):
                 turn_hidden(step - 1)
             if live(step - 2):
                 exponentials(step - 2)
             if live(step - 3):
-                sum_frames(step - 3, 1)
+                sum_weights(step - 3)
+                products(step - 3)
+                sum_products(step - 3)
             if closes_a_division(step - 3):
                 logarithms(division_of(step - 3))
             if closes_a_division(step - 4):

@@ -40,6 +40,7 @@ def tile_dwamformer_pa_t_kernel(tc, x, w1_words, w1_scales, w2_words, w2_scales,
         loads = stack.enter_context(tc.tile_pool(name="loads", bufs=4))
         work = stack.enter_context(tc.tile_pool(name="work", bufs=3))
         norm = stack.enter_context(tc.tile_pool(name="norm", bufs=2))
+        keep = stack.enter_context(tc.tile_pool(name="keep", bufs=NORM_ROUNDS + 3))
         psum = stack.enter_context(tc.psum_pool(name="psum", bufs=PSUM_BANKS))
 
         x_by_frame = {}
@@ -49,9 +50,9 @@ def tile_dwamformer_pa_t_kernel(tc, x, w1_words, w1_scales, w2_words, w2_scales,
         hidden = {}
         hidden_grouped = {}
         hidden_mx = {}
-        weights_and_products = {}
+        weights = {}
+        products_of = {}
         sums_of_weights = {}
-        sums_of_products = {}
 
         def load_weight(words, scales, label):
             codes = const.tile([P, D], U32, name=label + "_codes", align_bytes=64)
@@ -120,7 +121,7 @@ def tile_dwamformer_pa_t_kernel(tc, x, w1_words, w1_scales, w2_words, w2_scales,
                 )
                 dst = relu[:, t, :].rearrange("w (u p e) -> w u p e", u=2, e=2)
                 src = acc[:].rearrange("w (p u e) -> w u p e", u=2, e=2)
-                if t == 0:
+                if t % 2 == 0:
                     nc.vector.tensor_relu(out=dst, in_=src)
                 else:
                     nc.scalar.activation(out=dst, in_=src, func=ACT.Relu)
@@ -149,7 +150,7 @@ def tile_dwamformer_pa_t_kernel(tc, x, w1_words, w1_scales, w2_words, w2_scales,
 
         def second_matmul(r):
             codes, scales = hidden_mx[r]
-            both = work.tile([P, 2, TILES, MS, P], F32, name="weights_and_products")
+            gate = work.tile([P, TILES, MS, P], F32, name="weights")
             for t in range(TILES):
                 cols = slice(t * P, (t + 1) * P)
                 acc = psum.tile([P, D], F32, name="gate_acc", tag="bank")
@@ -163,66 +164,51 @@ def tile_dwamformer_pa_t_kernel(tc, x, w1_words, w1_scales, w2_words, w2_scales,
                     stop=True,
                 )
                 nc.scalar.activation(
-                    out=both[:, 0, t],
+                    out=gate[:, t],
                     in_=acc[:].rearrange("w (c m) -> w m c", m=MS),
                     func=ACT.Tanh,
                     scale=0.5,
                 )
-            weights_and_products[r] = both
+            weights[r] = gate
 
         def exponentials(r):
-            both = weights_and_products[r]
             for half in (slice(0, TILES // 2), slice(TILES // 2, TILES)):
                 nc.scalar.activation(
-                    out=both[:, 0, half], in_=both[:, 0, half], func=ACT.Exp, scale=0.5
+                    out=weights[r][:, half], in_=weights[r][:, half], func=ACT.Exp, scale=0.5
                 )
 
         def products(r):
-            both = weights_and_products[r]
+            weighted = keep.tile([P, TILES, MS, P], F32, name="products")
             nc.vector.tensor_tensor(
-                out=both[:, 1].rearrange("w t m c -> w t (m c)"),
-                in0=both[:, 0].rearrange("w t m c -> w t (m c)"),
+                out=weighted[:].rearrange("w t m c -> w t (m c)"),
+                in0=weights[r][:].rearrange("w t m c -> w t (m c)"),
                 in1=x_by_window[r][:],
                 op=ALU.mult,
             )
+            products_of[r] = weighted
 
-        def sum_weights(r):
-            if r == rounds_of(division_of(r))[0]:
-                fresh = norm.tile([P, NORM_ROUNDS, WINDOWS], F32, name="sums_of_weights")
-                sums_of_weights[division_of(r)] = fresh
-            both = weights_and_products[r]
-            turned = psum.tile([P, TILES, P], F32, name="weights_turned", tag="bank")
+        def add_frames(planes, label):
+            turned = psum.tile([P, TILES, P], F32, name=label, tag="bank")
             for t in range(TILES):
                 for m in range(MS):
                     nc.tensor.matmul(
                         out=turned[:, t, :],
-                        lhsT=both[:, 0, t, m, :],
+                        lhsT=planes[:, t, m, :],
                         rhs=identity_f32[:],
                         is_transpose=True,
                         start=(m == 0),
                         stop=(m == MS - 1),
                     )
+            return turned
+
+        def sum_weights(r):
+            if r == rounds_of(division_of(r))[0]:
+                fresh = norm.tile([P, NORM_ROUNDS, WINDOWS], F32, name="sums_of_weights")
+                sums_of_weights[division_of(r)] = fresh
+            turned = add_frames(weights[r], "weights_turned")
             nc.vector.tensor_copy(
                 out=sums_of_weights[division_of(r)][:, place_of(r), :],
                 in_=turned[:].rearrange("c t w -> c (t w)"),
-            )
-
-        def sum_products(r):
-            if r == rounds_of(division_of(r))[0]:
-                fresh = norm.tile([P, NORM_ROUNDS, WINDOWS], F32, name="sums_of_products")
-                sums_of_products[division_of(r)] = fresh
-            both = weights_and_products[r]
-            pairs = work.tile([P, TILES, 2, P], F32, name="pair_sums", bufs=2)
-            nc.vector.tensor_tensor(
-                out=pairs[:], in0=both[:, 1, :, 0:2, :], in1=both[:, 1, :, 2:4, :], op=ALU.add
-            )
-            nc.vector.tensor_tensor(
-                out=sums_of_products[division_of(r)][:, place_of(r), :].rearrange(
-                    "w (t c) -> w t c", t=TILES
-                ),
-                in0=pairs[:, :, 0, :],
-                in1=pairs[:, :, 1, :],
-                op=ALU.add,
             )
 
         def live(r):
@@ -247,23 +233,26 @@ def tile_dwamformer_pa_t_kernel(tc, x, w1_words, w1_scales, w2_words, w2_scales,
 
         def divide_and_store(n):
             for r in rounds_of(n):
-                cell = sums_of_weights[n][:, place_of(r), :]
-                nc.scalar.activation(out=cell, in_=cell, func=ACT.Exp, scale=-1.0)
-                inverse = psum.tile([P, TILES, P], F32, name="inverse", tag="bank")
-                for t in range(TILES):
-                    nc.tensor.transpose(
-                        inverse[:, t, :], cell[:, t * P : (t + 1) * P], identity_f32[:]
-                    )
-                pooled = norm.tile([P, WINDOWS], F32, name="pooled", bufs=3)
+                log_then_inverse = sums_of_weights[n][:, place_of(r), :]
+                nc.scalar.activation(
+                    out=log_then_inverse, in_=log_then_inverse, func=ACT.Exp, scale=-1.0
+                )
+                turned = add_frames(products_of[r], "products_turned")
+                pooled_turned = norm.tile([P, WINDOWS], F32, name="pooled_turned", bufs=3)
                 nc.vector.tensor_tensor(
-                    out=pooled[:],
-                    in0=sums_of_products[n][:, place_of(r), :],
-                    in1=inverse[:].rearrange("w t c -> w (t c)"),
+                    out=pooled_turned[:],
+                    in0=log_then_inverse,
+                    in1=turned[:].rearrange("c t w -> c (t w)"),
                     op=ALU.mult,
                 )
-                nc.sync.dma_start(
-                    out=out_by_round[r], in_=pooled[:].rearrange("w (t c) -> w t c", t=TILES)
-                )
+                back = psum.tile([P, TILES, P], F32, name="pooled_back", tag="bank")
+                for t in range(TILES):
+                    nc.tensor.transpose(
+                        back[:, t, :], pooled_turned[:, t * P : (t + 1) * P], identity_f32[:]
+                    )
+                pooled = norm.tile([P, TILES, P], F32, name="pooled", bufs=3)
+                nc.vector.tensor_copy(out=pooled[:], in_=back[:])
+                nc.sync.dma_start(out=out_by_round[r], in_=pooled[:])
 
         identity_bf16 = const.tile([P, P], BF16)
         make_identity(nc, identity_bf16[:])
@@ -295,7 +284,6 @@ def tile_dwamformer_pa_t_kernel(tc, x, w1_words, w1_scales, w2_words, w2_scales,
             if live(step - 3):
                 sum_weights(step - 3)
                 products(step - 3)
-                sum_products(step - 3)
             if closes_a_division(step - 3):
                 logarithms(division_of(step - 3))
             if closes_a_division(step - 4):

@@ -40,7 +40,6 @@ def tile_dwamformer_pa_t_kernel(tc, x, w1_words, w1_scales, w2_words, w2_scales,
         loads = stack.enter_context(tc.tile_pool(name="loads", bufs=4))
         work = stack.enter_context(tc.tile_pool(name="work", bufs=3))
         norm = stack.enter_context(tc.tile_pool(name="norm", bufs=2))
-        keep = stack.enter_context(tc.tile_pool(name="keep", bufs=NORM_ROUNDS + 3))
         psum = stack.enter_context(tc.psum_pool(name="psum", bufs=PSUM_BANKS))
 
         x_by_frame = {}
@@ -50,9 +49,9 @@ def tile_dwamformer_pa_t_kernel(tc, x, w1_words, w1_scales, w2_words, w2_scales,
         hidden = {}
         hidden_grouped = {}
         hidden_mx = {}
-        weights = {}
-        products_of = {}
-        sums_of_weights = {}
+        weights_and_products = {}
+        pair_sums = {}
+        totals = {}
 
         def load_weight(words, scales, label):
             codes = const.tile([P, D], U32, name=label + "_codes", align_bytes=64)
@@ -119,12 +118,11 @@ def tile_dwamformer_pa_t_kernel(tc, x, w1_words, w1_scales, w2_words, w2_scales,
                     start=True,
                     stop=True,
                 )
-                dst = relu[:, t, :].rearrange("w (u p e) -> w u p e", u=2, e=2)
-                src = acc[:].rearrange("w (p u e) -> w u p e", u=2, e=2)
-                if t % 2 == 0:
-                    nc.vector.tensor_relu(out=dst, in_=src)
-                else:
-                    nc.scalar.activation(out=dst, in_=src, func=ACT.Relu)
+                nc.scalar.activation(
+                    out=relu[:, t, :].rearrange("w (u p e) -> w u p e", u=2, e=2),
+                    in_=acc[:].rearrange("w (p u e) -> w u p e", u=2, e=2),
+                    func=ACT.Relu,
+                )
             hidden[r] = relu
 
         def turn_hidden(r):
@@ -145,12 +143,15 @@ def tile_dwamformer_pa_t_kernel(tc, x, w1_words, w1_scales, w2_words, w2_scales,
                     "p (t w u) -> p t w u", t=tiles_in_bank, u=2
                 )
                 src = turned[:].rearrange("p t u w -> p t w u")
-                nc.vector.tensor_copy(out=dst, in_=src)
+                if (r * (TILES // tiles_in_bank) + bank) % 4 == 3:
+                    nc.scalar.copy(out=dst, in_=src)
+                else:
+                    nc.vector.tensor_copy(out=dst, in_=src)
             hidden_grouped[r] = grouped
 
         def second_matmul(r):
             codes, scales = hidden_mx[r]
-            gate = work.tile([P, TILES, MS, P], F32, name="weights")
+            both = work.tile([P, 2, TILES, MS, P], F32, name="weights_and_products")
             for t in range(TILES):
                 cols = slice(t * P, (t + 1) * P)
                 acc = psum.tile([P, D], F32, name="gate_acc", tag="bank")
@@ -164,52 +165,36 @@ def tile_dwamformer_pa_t_kernel(tc, x, w1_words, w1_scales, w2_words, w2_scales,
                     stop=True,
                 )
                 nc.scalar.activation(
-                    out=gate[:, t],
+                    out=both[:, 0, t],
                     in_=acc[:].rearrange("w (c m) -> w m c", m=MS),
                     func=ACT.Tanh,
                     scale=0.5,
                 )
-            weights[r] = gate
+            weights_and_products[r] = both
 
         def exponentials(r):
+            both = weights_and_products[r]
             for half in (slice(0, TILES // 2), slice(TILES // 2, TILES)):
                 nc.scalar.activation(
-                    out=weights[r][:, half], in_=weights[r][:, half], func=ACT.Exp, scale=0.5
+                    out=both[:, 0, half], in_=both[:, 0, half], func=ACT.Exp, scale=0.5
                 )
 
         def products(r):
-            weighted = keep.tile([P, TILES, MS, P], F32, name="products")
+            both = weights_and_products[r]
             nc.vector.tensor_tensor(
-                out=weighted[:].rearrange("w t m c -> w t (m c)"),
-                in0=weights[r][:].rearrange("w t m c -> w t (m c)"),
+                out=both[:, 1].rearrange("w t m c -> w t (m c)"),
+                in0=both[:, 0].rearrange("w t m c -> w t (m c)"),
                 in1=x_by_window[r][:],
                 op=ALU.mult,
             )
-            products_of[r] = weighted
 
-        def add_frames(planes, label):
-            turned = psum.tile([P, TILES, P], F32, name=label, tag="bank")
-            for t in range(TILES):
-                for m in range(MS):
-                    nc.tensor.matmul(
-                        out=turned[:, t, :],
-                        lhsT=planes[:, t, m, :],
-                        rhs=identity_f32[:],
-                        is_transpose=True,
-                        start=(m == 0),
-                        stop=(m == MS - 1),
-                    )
-            return turned
-
-        def sum_weights(r):
-            if r == rounds_of(division_of(r))[0]:
-                fresh = norm.tile([P, NORM_ROUNDS, WINDOWS], F32, name="sums_of_weights")
-                sums_of_weights[division_of(r)] = fresh
-            turned = add_frames(weights[r], "weights_turned")
-            nc.vector.tensor_copy(
-                out=sums_of_weights[division_of(r)][:, place_of(r), :],
-                in_=turned[:].rearrange("c t w -> c (t w)"),
+        def sum_pairs(r):
+            both = weights_and_products[r][:].rearrange("w k t m c -> w (k t) m c")
+            pairs = work.tile([P, 2 * TILES, 2, P], F32, name="pair_sums", bufs=2)
+            nc.vector.tensor_tensor(
+                out=pairs[:], in0=both[:, :, 0:2, :], in1=both[:, :, 2:4, :], op=ALU.add
             )
+            pair_sums[r] = pairs
 
         def live(r):
             return 0 <= r < ROUNDS
@@ -226,33 +211,36 @@ def tile_dwamformer_pa_t_kernel(tc, x, w1_words, w1_scales, w2_words, w2_scales,
         def rounds_of(n):
             return [r for r in range(ROUNDS) if division_of(r) == n]
 
+        def sum_all(r):
+            if r == rounds_of(division_of(r))[0]:
+                fresh = norm.tile([P, 2, NORM_ROUNDS, WINDOWS], F32, name="totals")
+                totals[division_of(r)] = fresh
+            pairs = pair_sums[r]
+            nc.vector.tensor_tensor(
+                out=totals[division_of(r)][:, :, place_of(r), :].rearrange(
+                    "w k (t c) -> w k t c", t=TILES
+                ),
+                in0=pairs[:, :, 0, :].rearrange("w (k t) c -> w k t c", k=2),
+                in1=pairs[:, :, 1, :].rearrange("w (k t) c -> w k t c", k=2),
+                op=ALU.add,
+            )
+
         def logarithms(n):
             places = slice(place_of(rounds_of(n)[0]), place_of(rounds_of(n)[-1]) + 1)
-            sums = sums_of_weights[n][:, places, :]
+            sums = totals[n][:, 0, places, :]
             nc.scalar.activation(out=sums, in_=sums, func=ACT.Ln)
 
         def divide_and_store(n):
             for r in rounds_of(n):
-                log_then_inverse = sums_of_weights[n][:, place_of(r), :]
-                nc.scalar.activation(
-                    out=log_then_inverse, in_=log_then_inverse, func=ACT.Exp, scale=-1.0
-                )
-                turned = add_frames(products_of[r], "products_turned")
-                pooled_turned = norm.tile([P, WINDOWS], F32, name="pooled_turned", bufs=3)
+                log_of_sum = totals[n][:, 0, place_of(r), :]
+                nc.scalar.activation(out=log_of_sum, in_=log_of_sum, func=ACT.Exp, scale=-1.0)
+                pooled = norm.tile([P, WINDOWS], F32, name="pooled", bufs=3)
                 nc.vector.tensor_tensor(
-                    out=pooled_turned[:],
-                    in0=log_then_inverse,
-                    in1=turned[:].rearrange("c t w -> c (t w)"),
-                    op=ALU.mult,
+                    out=pooled[:], in0=totals[n][:, 1, place_of(r), :], in1=log_of_sum, op=ALU.mult
                 )
-                back = psum.tile([P, TILES, P], F32, name="pooled_back", tag="bank")
-                for t in range(TILES):
-                    nc.tensor.transpose(
-                        back[:, t, :], pooled_turned[:, t * P : (t + 1) * P], identity_f32[:]
-                    )
-                pooled = norm.tile([P, TILES, P], F32, name="pooled", bufs=3)
-                nc.vector.tensor_copy(out=pooled[:], in_=back[:])
-                nc.sync.dma_start(out=out_by_round[r], in_=pooled[:])
+                nc.sync.dma_start(
+                    out=out_by_round[r], in_=pooled[:].rearrange("w (t c) -> w t c", t=TILES)
+                )
 
         identity_bf16 = const.tile([P, P], BF16)
         make_identity(nc, identity_bf16[:])
@@ -282,8 +270,9 @@ def tile_dwamformer_pa_t_kernel(tc, x, w1_words, w1_scales, w2_words, w2_scales,
             if live(step - 2):
                 exponentials(step - 2)
             if live(step - 3):
-                sum_weights(step - 3)
                 products(step - 3)
+                sum_pairs(step - 3)
+                sum_all(step - 3)
             if closes_a_division(step - 3):
                 logarithms(division_of(step - 3))
             if closes_a_division(step - 4):

@@ -21,7 +21,6 @@ WINDOWS = TILES * P
 BLOCKS = WINDOWS * MS // P
 ROUNDS = WINDOWS_IN_ALL // WINDOWS
 BANK_BF16 = 1024
-BANK_F32 = 512
 NORM_ROUNDS = 6
 PSUM_BANKS = 8
 
@@ -32,7 +31,6 @@ def tile_dwamformer_pa_t_kernel(tc, x, w1_words, w1_scales, w2_words, w2_scales,
     nc = tc.nc
     frames = x.flatten_outer_dims()
     frames_by_round = frames.rearrange("(r b p) c -> r p b c", b=BLOCKS, p=P)
-    windows_by_round = frames.rearrange("(r t w m) c -> r w t (m c)", t=TILES, w=P, m=MS)
     out_by_round = out.flatten_outer_dims().rearrange("(r t w) c -> r w t c", t=TILES, w=P)
 
     with ExitStack() as stack:
@@ -43,41 +41,44 @@ def tile_dwamformer_pa_t_kernel(tc, x, w1_words, w1_scales, w2_words, w2_scales,
         psum = stack.enter_context(tc.psum_pool(name="psum", bufs=PSUM_BANKS))
 
         x_by_frame = {}
-        x_by_window = {}
         flat_grouped = {}
         flat_mx = {}
-        hidden = {}
         hidden_grouped = {}
         hidden_mx = {}
-        weights_and_products = {}
-        pair_sums = {}
+        weights = {}
+        weighted = {}
         totals = {}
 
         def load_weight(words, scales, label):
-            codes = const.tile([P, D], U32, name=label + "_codes", align_bytes=64)
+            raw_codes = const.tile([P, D], U32, name=label + "_raw_codes")
             nc.sync.dma_start(
-                out=codes[:].bitcast(I32),
+                out=raw_codes[:].bitcast(I32),
                 in_=words.rearrange("g p n t -> (g p) (n t)").bitcast(I32),
             )
-            plane = const.tile([P, D], U8, name=label + "_plane", align_bytes=64)
-            nc.vector.memset(plane[:].bitcast(I32), 0)
+            raw_plane = const.tile([P, D], U8, name=label + "_raw_plane")
+            nc.vector.memset(raw_plane[:].bitcast(I32), 0)
             rows = scales.rearrange("g q n -> (g q) n").bitcast(I32)
             for quadrant in range(4):
                 nc.sync.dma_start(
-                    out=plane[32 * quadrant : 32 * quadrant + 4, :].bitcast(I32),
+                    out=raw_plane[32 * quadrant : 32 * quadrant + 4, :].bitcast(I32),
                     in_=rows[4 * quadrant : 4 * quadrant + 4, :],
                 )
+            codes = const.tile([P, D], U32, name=label + "_codes", align_bytes=64)
+            nc.vector.tensor_copy(
+                out=codes[:].bitcast(I32).rearrange("p (t j) -> p t j", t=MS),
+                in_=raw_codes[:].bitcast(I32).rearrange("p (j t) -> p t j", t=MS),
+            )
+            plane = const.tile([P, D], U8, name=label + "_plane", align_bytes=64)
+            nc.vector.tensor_copy(
+                out=plane[:].rearrange("p (t j) -> p j t", t=MS),
+                in_=raw_plane[:].rearrange("p (j t) -> p j t", t=MS),
+            )
             return codes, plane
 
         def load_frames(r):
             by_frame = loads.tile([P, BLOCKS, P], BF16)
             nc.sync.dma_start(out=by_frame[:], in_=frames_by_round[r])
             x_by_frame[r] = by_frame
-
-        def load_windows(r):
-            by_window = loads.tile([P, TILES, D], BF16)
-            nc.sync.dma_start(out=by_window[:], in_=windows_by_round[r])
-            x_by_window[r] = by_window
 
         def quantise(grouped, label):
             codes = work.tile([P, WINDOWS], U32, name=label + "_codes", align_bytes=64)
@@ -86,7 +87,9 @@ def tile_dwamformer_pa_t_kernel(tc, x, w1_words, w1_scales, w2_words, w2_scales,
             return codes, scales
 
         def turn_frames(r):
-            grouped = work.tile([P, WINDOWS * MS], BF16, name="flat_grouped", align_bytes=64)
+            grouped = work.tile(
+                [P, WINDOWS * MS], BF16, name="flat_grouped", align_bytes=64, bufs=6
+            )
             blocks_in_bank = BANK_BF16 // P
             for bank in range(BLOCKS // blocks_in_bank):
                 turned = psum.tile([P, BANK_BF16], BF16, name="frames_turned", tag="bank")
@@ -96,105 +99,65 @@ def tile_dwamformer_pa_t_kernel(tc, x, w1_words, w1_scales, w2_words, w2_scales,
                         x_by_frame[r][:, bank * blocks_in_bank + b, :],
                         identity_bf16[:],
                     )
-                dst = grouped[:, bank * BANK_BF16 : (bank + 1) * BANK_BF16]
-                if bank % 2 == 0:
-                    nc.scalar.copy(out=dst, in_=turned[:])
-                else:
-                    nc.vector.tensor_copy(out=dst, in_=turned[:])
+                nc.scalar.copy(
+                    out=grouped[:, bank * BANK_BF16 : (bank + 1) * BANK_BF16], in_=turned[:]
+                )
             flat_grouped[r] = grouped
 
         def first_matmul(r):
             codes, scales = flat_mx[r]
-            relu = work.tile([P, TILES, D], BF16, name="hidden")
-            for t in range(TILES):
-                cols = slice(t * P, (t + 1) * P)
-                acc = psum.tile([P, D], F32, name="hidden_acc", tag="bank")
-                nc.tensor.matmul_mx(
-                    out=acc[:],
-                    lhsT=codes[:, cols].bitcast(FP8X4),
-                    lhsT_scale=scales[:, cols],
-                    rhs=w1_codes[:].bitcast(FP8X4),
-                    rhs_scale=w1_plane[:],
-                    start=True,
-                    stop=True,
-                )
-                nc.scalar.activation(
-                    out=relu[:, t, :].rearrange("w (u p e) -> w u p e", u=2, e=2),
-                    in_=acc[:].rearrange("w (p u e) -> w u p e", u=2, e=2),
-                    func=ACT.Relu,
-                )
-            hidden[r] = relu
-
-        def turn_hidden(r):
-            words = hidden[r][:].bitcast(F32)
             grouped = work.tile([P, WINDOWS * MS], BF16, name="hidden_grouped", align_bytes=64)
-            grouped_words = grouped[:].bitcast(F32)
-            tiles_in_bank = BANK_F32 // (2 * P)
-            for bank in range(TILES // tiles_in_bank):
-                turned = psum.tile([P, tiles_in_bank, 2, P], F32, name="hidden_turned", tag="bank")
-                for t in range(tiles_in_bank):
-                    for u in range(2):
-                        nc.tensor.transpose(
-                            turned[:, t, u, :],
-                            words[:, bank * tiles_in_bank + t, u * P : (u + 1) * P],
-                            identity_f32[:],
-                        )
-                dst = grouped_words[:, bank * BANK_F32 : (bank + 1) * BANK_F32].rearrange(
-                    "p (t w u) -> p t w u", t=tiles_in_bank, u=2
+            for tile in range(TILES):
+                cols = slice(tile * P, (tile + 1) * P)
+                acc = psum.tile([P, MS, P], F32, name="hidden_acc", tag="bank")
+                for t in range(MS):
+                    nc.tensor.matmul_mx(
+                        out=acc[:, t, :],
+                        lhsT=w1_codes[:, t * P : (t + 1) * P].bitcast(FP8X4),
+                        lhsT_scale=w1_plane[:, t * P : (t + 1) * P],
+                        rhs=codes[:, cols].bitcast(FP8X4),
+                        rhs_scale=scales[:, cols],
+                        start=True,
+                        stop=True,
+                    )
+                nc.vector.tensor_scalar_max(
+                    out=grouped[:, tile * D : (tile + 1) * D].rearrange("p (w t) -> p w t", t=MS),
+                    in0=acc[:].rearrange("p t w -> p w t"),
+                    scalar1=0.0,
                 )
-                src = turned[:].rearrange("p t u w -> p t w u")
-                if (r * (TILES // tiles_in_bank) + bank) % 4 == 3:
-                    nc.scalar.copy(out=dst, in_=src)
-                else:
-                    nc.vector.tensor_copy(out=dst, in_=src)
             hidden_grouped[r] = grouped
 
         def second_matmul(r):
             codes, scales = hidden_mx[r]
-            both = work.tile([P, 2, TILES, MS, P], F32, name="weights_and_products")
-            for t in range(TILES):
-                cols = slice(t * P, (t + 1) * P)
-                acc = psum.tile([P, D], F32, name="gate_acc", tag="bank")
+            gate = work.tile([P, MS, WINDOWS], F32, name="weights")
+            for m in range(MS):
+                acc = psum.tile([P, WINDOWS], F32, name="gate_acc", tag="bank")
                 nc.tensor.matmul_mx(
                     out=acc[:],
-                    lhsT=codes[:, cols].bitcast(FP8X4),
-                    lhsT_scale=scales[:, cols],
-                    rhs=w2_codes[:].bitcast(FP8X4),
-                    rhs_scale=w2_plane[:],
+                    lhsT=w2_codes[:, m * P : (m + 1) * P].bitcast(FP8X4),
+                    lhsT_scale=w2_plane[:, m * P : (m + 1) * P],
+                    rhs=codes[:].bitcast(FP8X4),
+                    rhs_scale=scales[:],
                     start=True,
                     stop=True,
                 )
-                nc.scalar.activation(
-                    out=both[:, 0, t],
-                    in_=acc[:].rearrange("w (c m) -> w m c", m=MS),
-                    func=ACT.Tanh,
-                    scale=0.5,
-                )
-            weights_and_products[r] = both
+                nc.scalar.activation(out=gate[:, m, :], in_=acc[:], func=ACT.Tanh, scale=0.5)
+            weights[r] = gate
 
         def exponentials(r):
-            both = weights_and_products[r]
-            for half in (slice(0, TILES // 2), slice(TILES // 2, TILES)):
-                nc.scalar.activation(
-                    out=both[:, 0, half], in_=both[:, 0, half], func=ACT.Exp, scale=0.5
-                )
+            gate = weights[r]
+            for half in (slice(0, MS // 2), slice(MS // 2, MS)):
+                nc.scalar.activation(out=gate[:, half], in_=gate[:, half], func=ACT.Exp, scale=0.5)
 
         def products(r):
-            both = weights_and_products[r]
+            product = work.tile([P, MS, WINDOWS], F32, name="weighted")
             nc.vector.tensor_tensor(
-                out=both[:, 1].rearrange("w t m c -> w t (m c)"),
-                in0=both[:, 0].rearrange("w t m c -> w t (m c)"),
-                in1=x_by_window[r][:],
+                out=product[:],
+                in0=weights[r][:],
+                in1=flat_grouped[r][:].rearrange("c (w m) -> c m w", m=MS),
                 op=ALU.mult,
             )
-
-        def sum_pairs(r):
-            both = weights_and_products[r][:].rearrange("w k t m c -> w (k t) m c")
-            pairs = work.tile([P, 2 * TILES, 2, P], F32, name="pair_sums", bufs=2)
-            nc.vector.tensor_tensor(
-                out=pairs[:], in0=both[:, :, 0:2, :], in1=both[:, :, 2:4, :], op=ALU.add
-            )
-            pair_sums[r] = pairs
+            weighted[r] = product
 
         def live(r):
             return 0 <= r < ROUNDS
@@ -211,18 +174,24 @@ def tile_dwamformer_pa_t_kernel(tc, x, w1_words, w1_scales, w2_words, w2_scales,
         def rounds_of(n):
             return [r for r in range(ROUNDS) if division_of(r) == n]
 
-        def sum_all(r):
-            if r == rounds_of(division_of(r))[0]:
+        def turn_and_add(r, terms, kind):
+            if kind == 0 and r == rounds_of(division_of(r))[0]:
                 fresh = norm.tile([P, 2, NORM_ROUNDS, WINDOWS], F32, name="totals")
                 totals[division_of(r)] = fresh
-            pairs = pair_sums[r]
-            nc.vector.tensor_tensor(
-                out=totals[division_of(r)][:, :, place_of(r), :].rearrange(
-                    "w k (t c) -> w k t c", t=TILES
-                ),
-                in0=pairs[:, :, 0, :].rearrange("w (k t) c -> w k t c", k=2),
-                in1=pairs[:, :, 1, :].rearrange("w (k t) c -> w k t c", k=2),
-                op=ALU.add,
+            acc = psum.tile([P, TILES, P], F32, name="frames_added", tag="bank")
+            for tile in range(TILES):
+                for m in range(MS):
+                    nc.tensor.matmul(
+                        out=acc[:, tile, :],
+                        lhsT=terms[:, m, tile * P : (tile + 1) * P],
+                        rhs=identity_f32[:],
+                        is_transpose=True,
+                        start=(m == 0),
+                        stop=(m == MS - 1),
+                    )
+            nc.vector.tensor_copy(
+                out=totals[division_of(r)][:, kind, place_of(r), :],
+                in_=acc[:].rearrange("w t c -> w (t c)"),
             )
 
         def logarithms(n):
@@ -252,27 +221,23 @@ def tile_dwamformer_pa_t_kernel(tc, x, w1_words, w1_scales, w2_words, w2_scales,
         load_frames(1)
         w2_codes, w2_plane = load_weight(w2_words, w2_scales, "w2")
 
-        for step in range(ROUNDS + 4):
+        for step in range(ROUNDS + 5):
             if live(step + 2):
                 load_frames(step + 2)
             if live(step - 2):
                 hidden_mx[step - 2] = quantise(hidden_grouped[step - 2], "hidden")
             if live(step):
-                load_windows(step)
                 turn_frames(step)
                 flat_mx[step] = quantise(flat_grouped[step], "flat")
             if live(step - 1):
                 first_matmul(step - 1)
             if live(step - 2):
                 second_matmul(step - 2)
-            if live(step - 1):
-                turn_hidden(step - 1)
-            if live(step - 2):
                 exponentials(step - 2)
             if live(step - 3):
+                turn_and_add(step - 3, weights[step - 3], 0)
                 products(step - 3)
-                sum_pairs(step - 3)
-                sum_all(step - 3)
+                turn_and_add(step - 3, weighted[step - 3], 1)
             if closes_a_division(step - 3):
                 logarithms(division_of(step - 3))
             if closes_a_division(step - 4):

@@ -23,6 +23,10 @@ ROUNDS = WINDOWS_IN_ALL // WINDOWS
 BANK_BF16 = 1024
 NORM_ROUNDS = 6
 PSUM_BANKS = 8
+BLOCKS_IN_BANK = BANK_BF16 // P
+FRAME_BANKS = BLOCKS // BLOCKS_IN_BANK
+LN_AFTER = 5
+DIVIDED_IN_A_STEP = 2
 
 FLOPS = 2 * 2 * WINDOWS_IN_ALL * D * D
 
@@ -41,12 +45,16 @@ def tile_dwamformer_pa_t_kernel(tc, x, w1_words, w1_scales, w2_words, w2_scales,
         psum = stack.enter_context(tc.psum_pool(name="psum", bufs=PSUM_BANKS))
 
         x_by_frame = {}
+        frames_turned = {}
         flat_grouped = {}
         flat_mx = {}
+        hidden_acc = {}
         hidden_grouped = {}
         hidden_mx = {}
+        gate_acc = {}
         weights = {}
         weighted = {}
+        frames_added = {}
         totals = {}
 
         def load_weight(words, scales, label):
@@ -86,78 +94,101 @@ def tile_dwamformer_pa_t_kernel(tc, x, w1_words, w1_scales, w2_words, w2_scales,
             nc.vector.quantize_mx(out=codes[:].bitcast(FP8X4), scales=scales[:], in_=grouped[:])
             return codes, scales
 
-        def turn_frames(r):
-            grouped = work.tile(
-                [P, WINDOWS * MS], BF16, name="flat_grouped", align_bytes=64, bufs=6
+        def quantise_flat(r):
+            flat_mx[r] = quantise(flat_grouped[r], "flat")
+
+        def quantise_hidden(r):
+            hidden_mx[r] = quantise(hidden_grouped[r], "hidden")
+
+        def turn_frames(r, bank):
+            turned = psum.tile([P, BANK_BF16], BF16, name="frames_turned", tag="bank")
+            for b in range(BLOCKS_IN_BANK):
+                nc.tensor.transpose(
+                    turned[:, b * P : (b + 1) * P],
+                    x_by_frame[r][:, bank * BLOCKS_IN_BANK + b, :],
+                    identity_bf16[:],
+                )
+            frames_turned[r, bank] = turned
+
+        def copy_frames(r, bank):
+            if bank == 0:
+                fresh = work.tile(
+                    [P, WINDOWS * MS], BF16, name="flat_grouped", align_bytes=64, bufs=8
+                )
+                flat_grouped[r] = fresh
+            nc.vector.tensor_copy(
+                out=flat_grouped[r][:, bank * BANK_BF16 : (bank + 1) * BANK_BF16],
+                in_=frames_turned[r, bank][:],
             )
-            blocks_in_bank = BANK_BF16 // P
-            for bank in range(BLOCKS // blocks_in_bank):
-                turned = psum.tile([P, BANK_BF16], BF16, name="frames_turned", tag="bank")
-                for b in range(blocks_in_bank):
-                    nc.tensor.transpose(
-                        turned[:, b * P : (b + 1) * P],
-                        x_by_frame[r][:, bank * blocks_in_bank + b, :],
-                        identity_bf16[:],
-                    )
-                nc.scalar.copy(
-                    out=grouped[:, bank * BANK_BF16 : (bank + 1) * BANK_BF16], in_=turned[:]
-                )
-            flat_grouped[r] = grouped
 
-        def first_matmul(r):
+        def first_matmul(r, tile):
             codes, scales = flat_mx[r]
-            grouped = work.tile([P, WINDOWS * MS], BF16, name="hidden_grouped", align_bytes=64)
-            for tile in range(TILES):
-                cols = slice(tile * P, (tile + 1) * P)
-                acc = psum.tile([P, MS, P], F32, name="hidden_acc", tag="bank")
-                for t in range(MS):
-                    nc.tensor.matmul_mx(
-                        out=acc[:, t, :],
-                        lhsT=w1_codes[:, t * P : (t + 1) * P].bitcast(FP8X4),
-                        lhsT_scale=w1_plane[:, t * P : (t + 1) * P],
-                        rhs=codes[:, cols].bitcast(FP8X4),
-                        rhs_scale=scales[:, cols],
-                        start=True,
-                        stop=True,
-                    )
-                nc.vector.tensor_scalar_max(
-                    out=grouped[:, tile * D : (tile + 1) * D].rearrange("p (w t) -> p w t", t=MS),
-                    in0=acc[:].rearrange("p t w -> p w t"),
-                    scalar1=0.0,
-                )
-            hidden_grouped[r] = grouped
-
-        def second_matmul(r):
-            codes, scales = hidden_mx[r]
-            gate = work.tile([P, MS, WINDOWS], F32, name="weights")
-            for m in range(MS):
-                acc = psum.tile([P, WINDOWS], F32, name="gate_acc", tag="bank")
+            cols = slice(tile * P, (tile + 1) * P)
+            acc = psum.tile([P, MS, P], F32, name="hidden_acc", tag="bank")
+            for t in range(MS):
                 nc.tensor.matmul_mx(
-                    out=acc[:],
-                    lhsT=w2_codes[:, m * P : (m + 1) * P].bitcast(FP8X4),
-                    lhsT_scale=w2_plane[:, m * P : (m + 1) * P],
-                    rhs=codes[:].bitcast(FP8X4),
-                    rhs_scale=scales[:],
+                    out=acc[:, t, :],
+                    lhsT=w1_codes[:, t * P : (t + 1) * P].bitcast(FP8X4),
+                    lhsT_scale=w1_plane[:, t * P : (t + 1) * P],
+                    rhs=codes[:, cols].bitcast(FP8X4),
+                    rhs_scale=scales[:, cols],
                     start=True,
                     stop=True,
                 )
-                nc.scalar.activation(out=gate[:, m, :], in_=acc[:], func=ACT.Tanh, scale=0.5)
-            weights[r] = gate
+            hidden_acc[r, tile] = acc
 
-        def exponentials(r):
-            gate = weights[r]
-            for half in (slice(0, MS // 2), slice(MS // 2, MS)):
-                nc.scalar.activation(out=gate[:, half], in_=gate[:, half], func=ACT.Exp, scale=0.5)
+        def relu(r, tile):
+            if tile == 0:
+                fresh = work.tile([P, WINDOWS * MS], BF16, name="hidden_grouped", align_bytes=64)
+                hidden_grouped[r] = fresh
+            dst = hidden_grouped[r][:, tile * D : (tile + 1) * D].rearrange(
+                "p (w t) -> p w t", t=MS
+            )
+            src = hidden_acc[r, tile][:].rearrange("p t w -> p w t")
+            if tile % 2 == 0:
+                nc.scalar.activation(out=dst, in_=src, func=ACT.Relu)
+            else:
+                nc.vector.tensor_scalar_max(out=dst, in0=src, scalar1=0.0)
 
-        def products(r):
-            product = work.tile([P, MS, WINDOWS], F32, name="weighted")
+        def second_matmul(r, m):
+            codes, scales = hidden_mx[r]
+            acc = psum.tile([P, WINDOWS], F32, name="gate_acc", tag="bank")
+            nc.tensor.matmul_mx(
+                out=acc[:],
+                lhsT=w2_codes[:, m * P : (m + 1) * P].bitcast(FP8X4),
+                lhsT_scale=w2_plane[:, m * P : (m + 1) * P],
+                rhs=codes[:].bitcast(FP8X4),
+                rhs_scale=scales[:],
+                start=True,
+                stop=True,
+            )
+            gate_acc[r, m] = acc
+
+        def tanh(r, m):
+            if m == 0:
+                fresh = work.tile([P, MS, WINDOWS], F32, name="weights", bufs=4)
+                weights[r] = fresh
+            nc.scalar.activation(
+                out=weights[r][:, m, :], in_=gate_acc[r, m][:], func=ACT.Tanh, scale=0.5
+            )
+
+        def pair(half):
+            return slice(2 * half, 2 * half + 2)
+
+        def exponentials(r, half):
+            part = weights[r][:, pair(half)]
+            nc.scalar.activation(out=part, in_=part, func=ACT.Exp, scale=0.5)
+
+        def products(r, half):
+            if half == 0:
+                fresh = work.tile([P, MS, WINDOWS], F32, name="weighted")
+                weighted[r] = fresh
             nc.vector.tensor_tensor(
-                out=product[:],
-                in0=weights[r][:],
-                in1=flat_grouped[r][:].rearrange("c (w m) -> c m w", m=MS),
+                out=weighted[r][:, pair(half)],
+                in0=weights[r][:, pair(half)],
+                in1=flat_grouped[r][:].rearrange("c (w m) -> c m w", m=MS)[:, pair(half)],
                 op=ALU.mult,
             )
-            weighted[r] = product
 
         def live(r):
             return 0 <= r < ROUNDS
@@ -168,16 +199,11 @@ def tile_dwamformer_pa_t_kernel(tc, x, w1_words, w1_scales, w2_words, w2_scales,
         def place_of(r):
             return r % NORM_ROUNDS
 
-        def closes_a_division(r):
-            return live(r) and (r == ROUNDS - 1 or division_of(r + 1) != division_of(r))
-
         def rounds_of(n):
             return [r for r in range(ROUNDS) if division_of(r) == n]
 
-        def turn_and_add(r, terms, kind):
-            if kind == 0 and r == rounds_of(division_of(r))[0]:
-                fresh = norm.tile([P, 2, NORM_ROUNDS, WINDOWS], F32, name="totals")
-                totals[division_of(r)] = fresh
+        def turn_and_add(r, kind):
+            terms = weighted[r] if kind == 1 else weights[r]
             acc = psum.tile([P, TILES, P], F32, name="frames_added", tag="bank")
             for tile in range(TILES):
                 for m in range(MS):
@@ -189,9 +215,15 @@ def tile_dwamformer_pa_t_kernel(tc, x, w1_words, w1_scales, w2_words, w2_scales,
                         start=(m == 0),
                         stop=(m == MS - 1),
                     )
+            frames_added[r, kind] = acc
+
+        def keep_sum(r, kind):
+            if kind == 0 and r == rounds_of(division_of(r))[0]:
+                fresh = norm.tile([P, 2, NORM_ROUNDS, WINDOWS], F32, name="totals")
+                totals[division_of(r)] = fresh
             nc.vector.tensor_copy(
                 out=totals[division_of(r)][:, kind, place_of(r), :],
-                in_=acc[:].rearrange("w t c -> w (t c)"),
+                in_=frames_added[r, kind][:].rearrange("w t c -> w (t c)"),
             )
 
         def logarithms(n):
@@ -199,17 +231,31 @@ def tile_dwamformer_pa_t_kernel(tc, x, w1_words, w1_scales, w2_words, w2_scales,
             sums = totals[n][:, 0, places, :]
             nc.scalar.activation(out=sums, in_=sums, func=ACT.Ln)
 
-        def divide_and_store(n):
-            for r in rounds_of(n):
-                log_of_sum = totals[n][:, 0, place_of(r), :]
-                nc.scalar.activation(out=log_of_sum, in_=log_of_sum, func=ACT.Exp, scale=-1.0)
-                pooled = norm.tile([P, WINDOWS], F32, name="pooled", bufs=3)
-                nc.vector.tensor_tensor(
-                    out=pooled[:], in0=totals[n][:, 1, place_of(r), :], in1=log_of_sum, op=ALU.mult
-                )
-                nc.sync.dma_start(
-                    out=out_by_round[r], in_=pooled[:].rearrange("w (t c) -> w t c", t=TILES)
-                )
+        def divide_and_store(r):
+            n = division_of(r)
+            log_of_sum = totals[n][:, 0, place_of(r), :]
+            nc.scalar.activation(out=log_of_sum, in_=log_of_sum, func=ACT.Exp, scale=-1.0)
+            pooled = norm.tile([P, WINDOWS], F32, name="pooled", bufs=6)
+            nc.vector.tensor_tensor(
+                out=pooled[:], in0=totals[n][:, 1, place_of(r), :], in1=log_of_sum, op=ALU.mult
+            )
+            nc.sync.dma_start(
+                out=out_by_round[r], in_=pooled[:].rearrange("w (t c) -> w t c", t=TILES)
+            )
+
+        def divisions(step):
+            for n in range(division_of(ROUNDS - 1) + 1):
+                rounds = rounds_of(n)
+                first_step = rounds[-1] + LN_AFTER
+                is_last = rounds[-1] == ROUNDS - 1
+                if step == first_step:
+                    logarithms(n)
+                for place, r in enumerate(rounds):
+                    if is_last:
+                        if step == first_step:
+                            divide_and_store(r)
+                    elif step == first_step + 1 + place // DIVIDED_IN_A_STEP:
+                        divide_and_store(r)
 
         identity_bf16 = const.tile([P, P], BF16)
         make_identity(nc, identity_bf16[:])
@@ -221,24 +267,20 @@ def tile_dwamformer_pa_t_kernel(tc, x, w1_words, w1_scales, w2_words, w2_scales,
         load_frames(1)
         w2_codes, w2_plane = load_weight(w2_words, w2_scales, "w2")
 
-        for step in range(ROUNDS + 5):
-            if live(step + 2):
-                load_frames(step + 2)
-            if live(step - 2):
-                hidden_mx[step - 2] = quantise(hidden_grouped[step - 2], "hidden")
-            if live(step):
-                turn_frames(step)
-                flat_mx[step] = quantise(flat_grouped[step], "flat")
-            if live(step - 1):
-                first_matmul(step - 1)
-            if live(step - 2):
-                second_matmul(step - 2)
-                exponentials(step - 2)
-            if live(step - 3):
-                turn_and_add(step - 3, weights[step - 3], 0)
-                products(step - 3)
-                turn_and_add(step - 3, weighted[step - 3], 1)
-            if closes_a_division(step - 3):
-                logarithms(division_of(step - 3))
-            if closes_a_division(step - 4):
-                divide_and_store(division_of(step - 4))
+        step_text = [(load_frames, -2, ()), (products, 4, (1,)), (quantise_hidden, 2, ())]
+        step_text += [(turn_frames, 0, (bank,)) for bank in range(FRAME_BANKS)]
+        step_text += [(copy_frames, 0, (bank,)) for bank in range(FRAME_BANKS)]
+        for tile in range(TILES):
+            step_text += [(first_matmul, 1, (tile,)), (relu, 1, (tile,))]
+        for m in range(MS):
+            step_text += [(second_matmul, 2, (m,)), (tanh, 2, (m,))]
+        step_text += [(exponentials, 2, (0,)), (exponentials, 2, (1,))]
+        step_text += [(turn_and_add, 3, (0,)), (products, 3, (0,)), (keep_sum, 3, (0,))]
+        step_text += [(quantise_flat, 0, ()), (turn_and_add, 4, (1,)), (keep_sum, 4, (1,))]
+
+        stack.enter_context(tc.manual_schedule())
+        for step in range(ROUNDS + LN_AFTER + 1):
+            for stage, steps_after, arguments in step_text:
+                if live(step - steps_after):
+                    stage(step - steps_after, *arguments)
+            divisions(step)

@@ -25,7 +25,7 @@ NORM_ROUNDS = 6
 PSUM_BANKS = 8
 BLOCKS_IN_BANK = BANK_BF16 // P
 FRAME_BANKS = BLOCKS // BLOCKS_IN_BANK
-LN_AFTER = 5
+LN_AFTER = 6
 DIVIDED_IN_A_STEP = 2
 
 FLOPS = 2 * 2 * WINDOWS_IN_ALL * D * D
@@ -267,7 +267,7 @@ def tile_dwamformer_pa_t_kernel(tc, x, w1_words, w1_scales, w2_words, w2_scales,
         load_frames(1)
         w2_codes, w2_plane = load_weight(w2_words, w2_scales, "w2")
 
-        step_text = [(load_frames, -2, ()), (products, 4, (1,)), (quantise_hidden, 2, ())]
+        step_text = [(load_frames, -2, ()), (products, 4, (1,)), (keep_sum, 5, (1,))]
         step_text += [(turn_frames, 0, (bank,)) for bank in range(FRAME_BANKS)]
         step_text += [(copy_frames, 0, (bank,)) for bank in range(FRAME_BANKS)]
         for tile in range(TILES):
@@ -275,8 +275,8 @@ def tile_dwamformer_pa_t_kernel(tc, x, w1_words, w1_scales, w2_words, w2_scales,
         for m in range(MS):
             step_text += [(second_matmul, 2, (m,)), (tanh, 2, (m,))]
         step_text += [(exponentials, 2, (0,)), (exponentials, 2, (1,))]
-        step_text += [(turn_and_add, 3, (0,)), (products, 3, (0,)), (keep_sum, 3, (0,))]
-        step_text += [(quantise_flat, 0, ()), (turn_and_add, 4, (1,)), (keep_sum, 4, (1,))]
+        step_text += [(turn_and_add, 3, (0,)), (products, 3, (0,)), (quantise_flat, 0, ())]
+        step_text += [(keep_sum, 3, (0,)), (quantise_hidden, 1, ()), (turn_and_add, 4, (1,))]
 
         stack.enter_context(tc.manual_schedule())
         for step in range(ROUNDS + LN_AFTER + 1):

@@ -21,11 +21,11 @@ WINDOWS = TILES * P
 BLOCKS = WINDOWS * MS // P
 ROUNDS = WINDOWS_IN_ALL // WINDOWS
 BANK_BF16 = 1024
-NORM_ROUNDS = 6
+DIVISIONS = (9, 5, 2)
 PSUM_BANKS = 8
 BLOCKS_IN_BANK = BANK_BF16 // P
 FRAME_BANKS = BLOCKS // BLOCKS_IN_BANK
-LN_AFTER = 6
+LN_AFTER = 4
 DIVIDED_IN_A_STEP = 2
 
 FLOPS = 2 * 2 * WINDOWS_IN_ALL * D * D
@@ -137,7 +137,7 @@ def tile_dwamformer_pa_t_kernel(tc, x, w1_words, w1_scales, w2_words, w2_scales,
                 )
             hidden_acc[r, tile] = acc
 
-        def relu(r, tile):
+        def relu(r, tile, step):
             if tile == 0:
                 fresh = work.tile([P, WINDOWS * MS], BF16, name="hidden_grouped", align_bytes=64)
                 hidden_grouped[r] = fresh
@@ -145,7 +145,7 @@ def tile_dwamformer_pa_t_kernel(tc, x, w1_words, w1_scales, w2_words, w2_scales,
                 "p (w t) -> p w t", t=MS
             )
             src = hidden_acc[r, tile][:].rearrange("p t w -> p w t")
-            if tile % 2 == 0:
+            if tile % 2 == 0 and not scalar_divides(step):
                 nc.scalar.activation(out=dst, in_=src, func=ACT.Relu)
             else:
                 nc.vector.tensor_scalar_max(out=dst, in0=src, scalar1=0.0)
@@ -193,14 +193,31 @@ def tile_dwamformer_pa_t_kernel(tc, x, w1_words, w1_scales, w2_words, w2_scales,
         def live(r):
             return 0 <= r < ROUNDS
 
+        def rounds_of(n):
+            first = sum(DIVISIONS[:n])
+            return list(range(first, first + DIVISIONS[n]))
+
         def division_of(r):
-            return r // NORM_ROUNDS
+            return [n for n in range(len(DIVISIONS)) if r in rounds_of(n)][0]
 
         def place_of(r):
-            return r % NORM_ROUNDS
+            return r - rounds_of(division_of(r))[0]
 
-        def rounds_of(n):
-            return [r for r in range(ROUNDS) if division_of(r) == n]
+        def step_of_logarithms(n):
+            return rounds_of(n)[-1] + LN_AFTER
+
+        def step_of_inverse(r):
+            n = division_of(r)
+            if n == len(DIVISIONS) - 1:
+                return step_of_logarithms(n)
+            return step_of_logarithms(n) + 1 + place_of(r) // DIVIDED_IN_A_STEP
+
+        def scalar_divides(step):
+            after_logarithms = any(
+                step in (step_of_logarithms(n), step_of_logarithms(n) + 1)
+                for n in range(len(DIVISIONS))
+            )
+            return after_logarithms or any(step == step_of_inverse(r) for r in range(ROUNDS))
 
         def turn_and_add(r, kind):
             terms = weighted[r] if kind == 1 else weights[r]
@@ -217,45 +234,44 @@ def tile_dwamformer_pa_t_kernel(tc, x, w1_words, w1_scales, w2_words, w2_scales,
                     )
             frames_added[r, kind] = acc
 
-        def keep_sum(r, kind):
-            if kind == 0 and r == rounds_of(division_of(r))[0]:
-                fresh = norm.tile([P, 2, NORM_ROUNDS, WINDOWS], F32, name="totals")
-                totals[division_of(r)] = fresh
-            nc.vector.tensor_copy(
-                out=totals[division_of(r)][:, kind, place_of(r), :],
-                in_=frames_added[r, kind][:].rearrange("w t c -> w (t c)"),
-            )
-
-        def logarithms(n):
-            places = slice(place_of(rounds_of(n)[0]), place_of(rounds_of(n)[-1]) + 1)
-            sums = totals[n][:, 0, places, :]
-            nc.scalar.activation(out=sums, in_=sums, func=ACT.Ln)
-
-        def divide_and_store(r):
+        def keep_sum(r, kind, step):
             n = division_of(r)
-            log_of_sum = totals[n][:, 0, place_of(r), :]
-            nc.scalar.activation(out=log_of_sum, in_=log_of_sum, func=ACT.Exp, scale=-1.0)
-            pooled = norm.tile([P, WINDOWS], F32, name="pooled", bufs=6)
-            nc.vector.tensor_tensor(
-                out=pooled[:], in0=totals[n][:, 1, place_of(r), :], in1=log_of_sum, op=ALU.mult
-            )
-            nc.sync.dma_start(
-                out=out_by_round[r], in_=pooled[:].rearrange("w (t c) -> w t c", t=TILES)
-            )
+            if kind == 0 and place_of(r) == 0:
+                fresh = const.tile([P, 2, DIVISIONS[n], WINDOWS], F32, name="totals_%d" % n)
+                totals[n] = fresh
+            dst = totals[n][:, kind, place_of(r), :]
+            src = frames_added[r, kind][:].rearrange("w t c -> w (t c)")
+            if kind == 0 and not scalar_divides(step):
+                nc.scalar.copy(out=dst, in_=src)
+            else:
+                nc.vector.tensor_copy(out=dst, in_=src)
 
-        def divisions(step):
-            for n in range(division_of(ROUNDS - 1) + 1):
-                rounds = rounds_of(n)
-                first_step = rounds[-1] + LN_AFTER
-                is_last = rounds[-1] == ROUNDS - 1
-                if step == first_step:
-                    logarithms(n)
-                for place, r in enumerate(rounds):
-                    if is_last:
-                        if step == first_step:
-                            divide_and_store(r)
-                    elif step == first_step + 1 + place // DIVIDED_IN_A_STEP:
-                        divide_and_store(r)
+        def logarithms(step):
+            for n in range(len(DIVISIONS)):
+                if step == step_of_logarithms(n):
+                    sums = totals[n][:, 0]
+                    nc.scalar.activation(out=sums, in_=sums, func=ACT.Ln)
+
+        def inverses(step):
+            for r in range(ROUNDS):
+                if step == step_of_inverse(r):
+                    log_of_sum = totals[division_of(r)][:, 0, place_of(r), :]
+                    nc.scalar.activation(out=log_of_sum, in_=log_of_sum, func=ACT.Exp, scale=-1.0)
+
+        def divide_and_store(step):
+            for r in range(ROUNDS):
+                if step == step_of_inverse(r) + 1:
+                    both = totals[division_of(r)]
+                    pooled = norm.tile([P, WINDOWS], F32, name="pooled", bufs=6)
+                    nc.vector.tensor_tensor(
+                        out=pooled[:],
+                        in0=both[:, 1, place_of(r), :],
+                        in1=both[:, 0, place_of(r), :],
+                        op=ALU.mult,
+                    )
+                    nc.sync.dma_start(
+                        out=out_by_round[r], in_=pooled[:].rearrange("w (t c) -> w t c", t=TILES)
+                    )
 
         identity_bf16 = const.tile([P, P], BF16)
         make_identity(nc, identity_bf16[:])
@@ -275,12 +291,19 @@ def tile_dwamformer_pa_t_kernel(tc, x, w1_words, w1_scales, w2_words, w2_scales,
         for m in range(MS):
             step_text += [(second_matmul, 2, (m,)), (tanh, 2, (m,))]
         step_text += [(exponentials, 2, (0,)), (exponentials, 2, (1,))]
-        step_text += [(turn_and_add, 3, (0,)), (products, 3, (0,)), (quantise_flat, 0, ())]
-        step_text += [(keep_sum, 3, (0,)), (quantise_hidden, 1, ()), (turn_and_add, 4, (1,))]
+        step_text += [(logarithms, None, ()), (inverses, None, ())]
+        step_text += [(turn_and_add, 3, (0,)), (products, 3, (0,)), (divide_and_store, None, ())]
+        step_text += [(quantise_flat, 0, ()), (keep_sum, 3, (0,)), (quantise_hidden, 1, ())]
+        step_text += [(turn_and_add, 4, (1,))]
+        needs_step = (relu, keep_sum)
 
         stack.enter_context(tc.manual_schedule())
-        for step in range(ROUNDS + LN_AFTER + 1):
+        for step in range(ROUNDS + LN_AFTER + 2):
             for stage, steps_after, arguments in step_text:
-                if live(step - steps_after):
-                    stage(step - steps_after, *arguments)
-            divisions(step)
+                if steps_after is None:
+                    stage(step)
+                elif live(step - steps_after):
+                    if stage in needs_step:
+                        stage(step - steps_after, *arguments, step)
+                    else:
+                        stage(step - steps_after, *arguments)

@@ -180,15 +180,25 @@ def tile_dwamformer_pa_t_kernel(tc, x, w1_words, w1_scales, w2_words, w2_scales,
             nc.scalar.activation(out=part, in_=part, func=ACT.Exp, scale=0.5)
 
         def products(r, half):
-            if half == 0:
+            if r not in weighted:
                 fresh = work.tile([P, MS, WINDOWS], F32, name="weighted")
                 weighted[r] = fresh
-            nc.vector.tensor_tensor(
-                out=weighted[r][:, pair(half)],
-                in0=weights[r][:, pair(half)],
-                in1=flat_grouped[r][:].rearrange("c (w m) -> c m w", m=MS)[:, pair(half)],
-                op=ALU.mult,
-            )
+            by_frame = flat_grouped[r][:].rearrange("c (w m) -> c m w", m=MS)
+            if half == 0:
+                nc.vector.tensor_tensor(
+                    out=weighted[r][:, pair(half)],
+                    in0=weights[r][:, pair(half)],
+                    in1=by_frame[:, pair(half)],
+                    op=ALU.mult,
+                )
+            else:
+                for m in range(2 * half, 2 * half + 2):
+                    nc.gpsimd.tensor_tensor(
+                        out=weighted[r][:, m, :],
+                        in0=weights[r][:, m, :],
+                        in1=by_frame[:, m, :],
+                        op=ALU.mult,
+                    )
 
         def live(r):
             return 0 <= r < ROUNDS
@@ -234,17 +244,14 @@ def tile_dwamformer_pa_t_kernel(tc, x, w1_words, w1_scales, w2_words, w2_scales,
                     )
             frames_added[r, kind] = acc
 
-        def keep_sum(r, kind, step):
+        def keep_sum(r, kind):
             n = division_of(r)
             if kind == 0 and place_of(r) == 0:
                 fresh = const.tile([P, 2, DIVISIONS[n], WINDOWS], F32, name="totals_%d" % n)
                 totals[n] = fresh
             dst = totals[n][:, kind, place_of(r), :]
             src = frames_added[r, kind][:].rearrange("w t c -> w (t c)")
-            if kind == 0 and not scalar_divides(step):
-                nc.scalar.copy(out=dst, in_=src)
-            else:
-                nc.vector.tensor_copy(out=dst, in_=src)
+            nc.vector.tensor_copy(out=dst, in_=src)
 
         def logarithms(step):
             for n in range(len(DIVISIONS)):
@@ -283,7 +290,7 @@ def tile_dwamformer_pa_t_kernel(tc, x, w1_words, w1_scales, w2_words, w2_scales,
         load_frames(1)
         w2_codes, w2_plane = load_weight(w2_words, w2_scales, "w2")
 
-        step_text = [(load_frames, -2, ()), (products, 4, (1,)), (keep_sum, 5, (1,))]
+        step_text = [(load_frames, -2, ()), (products, 3, (1,)), (keep_sum, 5, (1,))]
         step_text += [(turn_frames, 0, (bank,)) for bank in range(FRAME_BANKS)]
         step_text += [(copy_frames, 0, (bank,)) for bank in range(FRAME_BANKS)]
         for tile in range(TILES):
@@ -295,7 +302,7 @@ def tile_dwamformer_pa_t_kernel(tc, x, w1_words, w1_scales, w2_words, w2_scales,
         step_text += [(turn_and_add, 3, (0,)), (products, 3, (0,)), (divide_and_store, None, ())]
         step_text += [(quantise_flat, 0, ()), (keep_sum, 3, (0,)), (quantise_hidden, 1, ())]
         step_text += [(turn_and_add, 4, (1,))]
-        needs_step = (relu, keep_sum)
+        needs_step = (relu,)
 
         stack.enter_context(tc.manual_schedule())
         for step in range(ROUNDS + LN_AFTER + 2):

@@ -21,7 +21,7 @@ WINDOWS = TILES * P
 BLOCKS = WINDOWS * MS // P
 ROUNDS = WINDOWS_IN_ALL // WINDOWS
 BANK_BF16 = 1024
-DIVISIONS = (9, 5, 2)
+DIVISIONS = (10, 5)
 PSUM_BANKS = 8
 BLOCKS_IN_BANK = BANK_BF16 // P
 FRAME_BANKS = BLOCKS // BLOCKS_IN_BANK
@@ -56,6 +56,7 @@ def tile_dwamformer_pa_t_kernel(tc, x, w1_words, w1_scales, w2_words, w2_scales,
         weighted = {}
         frames_added = {}
         totals = {}
+        inverse = {}
 
         def load_weight(words, scales, label):
             raw_codes = const.tile([P, D], U32, name=label + "_raw_codes")
@@ -210,6 +211,9 @@ def tile_dwamformer_pa_t_kernel(tc, x, w1_words, w1_scales, w2_words, w2_scales,
         def division_of(r):
             return [n for n in range(len(DIVISIONS)) if r in rounds_of(n)][0]
 
+        def divided_by_scalar(r):
+            return r < sum(DIVISIONS)
+
         def place_of(r):
             return r - rounds_of(division_of(r))[0]
 
@@ -227,7 +231,9 @@ def tile_dwamformer_pa_t_kernel(tc, x, w1_words, w1_scales, w2_words, w2_scales,
                 step in (step_of_logarithms(n), step_of_logarithms(n) + 1)
                 for n in range(len(DIVISIONS))
             )
-            return after_logarithms or any(step == step_of_inverse(r) for r in range(ROUNDS))
+            return after_logarithms or any(
+                step == step_of_inverse(r) for r in range(sum(DIVISIONS))
+            )
 
         def turn_and_add(r, kind):
             terms = weighted[r] if kind == 1 else weights[r]
@@ -244,13 +250,28 @@ def tile_dwamformer_pa_t_kernel(tc, x, w1_words, w1_scales, w2_words, w2_scales,
                     )
             frames_added[r, kind] = acc
 
+        def store(r, pooled):
+            nc.sync.dma_start(
+                out=out_by_round[r], in_=pooled[:].rearrange("w (t c) -> w t c", t=TILES)
+            )
+
         def keep_sum(r, kind):
+            src = frames_added[r, kind][:].rearrange("w t c -> w (t c)")
+            if not divided_by_scalar(r):
+                if kind == 0:
+                    fresh = norm.tile([P, WINDOWS], F32, name="inverse")
+                    nc.vector.reciprocal(out=fresh[:], in_=src)
+                    inverse[r] = fresh
+                else:
+                    pooled = norm.tile([P, WINDOWS], F32, name="pooled", bufs=6)
+                    nc.vector.tensor_tensor(out=pooled[:], in0=src, in1=inverse[r][:], op=ALU.mult)
+                    store(r, pooled)
+                return
             n = division_of(r)
             if kind == 0 and place_of(r) == 0:
                 fresh = const.tile([P, 2, DIVISIONS[n], WINDOWS], F32, name="totals_%d" % n)
                 totals[n] = fresh
             dst = totals[n][:, kind, place_of(r), :]
-            src = frames_added[r, kind][:].rearrange("w t c -> w (t c)")
             nc.vector.tensor_copy(out=dst, in_=src)
 
         def logarithms(step):
@@ -260,13 +281,13 @@ def tile_dwamformer_pa_t_kernel(tc, x, w1_words, w1_scales, w2_words, w2_scales,
                     nc.scalar.activation(out=sums, in_=sums, func=ACT.Ln)
 
         def inverses(step):
-            for r in range(ROUNDS):
+            for r in range(sum(DIVISIONS)):
                 if step == step_of_inverse(r):
                     log_of_sum = totals[division_of(r)][:, 0, place_of(r), :]
                     nc.scalar.activation(out=log_of_sum, in_=log_of_sum, func=ACT.Exp, scale=-1.0)
 
         def divide_and_store(step):
-            for r in range(ROUNDS):
+            for r in range(sum(DIVISIONS)):
                 if step == step_of_inverse(r) + 1:
                     both = totals[division_of(r)]
                     pooled = norm.tile([P, WINDOWS], F32, name="pooled", bufs=6)
@@ -276,9 +297,7 @@ def tile_dwamformer_pa_t_kernel(tc, x, w1_words, w1_scales, w2_words, w2_scales,
                         in1=both[:, 0, place_of(r), :],
                         op=ALU.mult,
                     )
-                    nc.sync.dma_start(
-                        out=out_by_round[r], in_=pooled[:].rearrange("w (t c) -> w t c", t=TILES)
-                    )
+                    store(r, pooled)
 
         identity_bf16 = const.tile([P, P], BF16)
         make_identity(nc, identity_bf16[:])
@@ -305,7 +324,7 @@ def tile_dwamformer_pa_t_kernel(tc, x, w1_words, w1_scales, w2_words, w2_scales,
         needs_step = (relu,)
 
         stack.enter_context(tc.manual_schedule())
-        for step in range(ROUNDS + LN_AFTER + 2):
+        for step in range(ROUNDS + 6):
             for stage, steps_after, arguments in step_text:
                 if steps_after is None:
                     stage(step)

@@ -21,7 +21,7 @@ WINDOWS = TILES * P
 BLOCKS = WINDOWS * MS // P
 ROUNDS = WINDOWS_IN_ALL // WINDOWS
 BANK_BF16 = 1024
-DIVISIONS = (10, 5)
+DIVISIONS = (4, 6, 5)
 PSUM_BANKS = 8
 BLOCKS_IN_BANK = BANK_BF16 // P
 FRAME_BANKS = BLOCKS // BLOCKS_IN_BANK

@@ -16,32 +16,32 @@ P = 128
 MS = 4
 D = P * MS
 WINDOWS_IN_ALL = 8 * 1024
-TILES = 4
-WINDOWS = TILES * P
-BLOCKS = WINDOWS * MS // P
-ROUNDS = WINDOWS_IN_ALL // WINDOWS
 BANK_BF16 = 1024
-DIVISIONS = (4, 6, 5)
 PSUM_BANKS = 8
 BLOCKS_IN_BANK = BANK_BF16 // P
-FRAME_BANKS = BLOCKS // BLOCKS_IN_BANK
-LN_AFTER = 4
-DIVIDED_IN_A_STEP = 2
+TILES_IN_BANK = BLOCKS_IN_BANK // MS
+ROUND_TILES = (2,) + (4,) * 15 + (2,)
+ROUNDS = len(ROUND_TILES)
+GROUPS = ((0, 1, 2, 3, 4, 5, 6, 7, 8, 9), (10, 11, 12, 13, 14, 15, 16))
 
 FLOPS = 2 * 2 * WINDOWS_IN_ALL * D * D
 
 
 def tile_dwamformer_pa_t_kernel(tc, x, w1_words, w1_scales, w2_words, w2_scales, out):
     nc = tc.nc
-    frames = x.flatten_outer_dims()
-    frames_by_round = frames.rearrange("(r b p) c -> r p b c", b=BLOCKS, p=P)
-    out_by_round = out.flatten_outer_dims().rearrange("(r t w) c -> r w t c", t=TILES, w=P)
+    frames = x.flatten_outer_dims().rearrange("(b p) c -> p b c", p=P)
+    windows = out.flatten_outer_dims().rearrange("(t w) c -> w t c", w=P)
+
+    def first_tile(r):
+        return sum(ROUND_TILES[:r])
+
+    def columns(r):
+        return ROUND_TILES[r] * P
 
     with ExitStack() as stack:
         const = stack.enter_context(tc.tile_pool(name="const", bufs=1))
         loads = stack.enter_context(tc.tile_pool(name="loads", bufs=4))
         work = stack.enter_context(tc.tile_pool(name="work", bufs=3))
-        norm = stack.enter_context(tc.tile_pool(name="norm", bufs=2))
         psum = stack.enter_context(tc.psum_pool(name="psum", bufs=PSUM_BANKS))
 
         x_by_frame = {}
@@ -56,7 +56,18 @@ def tile_dwamformer_pa_t_kernel(tc, x, w1_words, w1_scales, w2_words, w2_scales,
         weighted = {}
         frames_added = {}
         totals = {}
-        inverse = {}
+
+        def load_frames(r, pieces=1):
+            tiles = ROUND_TILES[r]
+            by_frame = loads.tile([P, MS * MS, P], BF16, name="by_frame")
+            step = tiles * MS // pieces
+            for first in range(0, tiles * MS, step):
+                source = first_tile(r) * MS + first
+                nc.sync.dma_start(
+                    out=by_frame[:, first : first + step, :],
+                    in_=frames[:, source : source + step, :],
+                )
+            x_by_frame[r] = by_frame
 
         def load_weight(words, scales, label):
             raw_codes = const.tile([P, D], U32, name=label + "_raw_codes")
@@ -64,14 +75,15 @@ def tile_dwamformer_pa_t_kernel(tc, x, w1_words, w1_scales, w2_words, w2_scales,
                 out=raw_codes[:].bitcast(I32),
                 in_=words.rearrange("g p n t -> (g p) (n t)").bitcast(I32),
             )
-            raw_plane = const.tile([P, D], U8, name=label + "_raw_plane")
-            nc.vector.memset(raw_plane[:].bitcast(I32), 0)
             rows = scales.rearrange("g q n -> (g q) n").bitcast(I32)
             for quadrant in range(4):
                 nc.sync.dma_start(
-                    out=raw_plane[32 * quadrant : 32 * quadrant + 4, :].bitcast(I32),
+                    out=raw_plane[label][32 * quadrant : 32 * quadrant + 4, :].bitcast(I32),
                     in_=rows[4 * quadrant : 4 * quadrant + 4, :],
                 )
+            return raw_codes
+
+        def regroup_weight(raw_codes, label):
             codes = const.tile([P, D], U32, name=label + "_codes", align_bytes=64)
             nc.vector.tensor_copy(
                 out=codes[:].bitcast(I32).rearrange("p (t j) -> p t j", t=MS),
@@ -80,26 +92,18 @@ def tile_dwamformer_pa_t_kernel(tc, x, w1_words, w1_scales, w2_words, w2_scales,
             plane = const.tile([P, D], U8, name=label + "_plane", align_bytes=64)
             nc.vector.tensor_copy(
                 out=plane[:].rearrange("p (t j) -> p j t", t=MS),
-                in_=raw_plane[:].rearrange("p (j t) -> p j t", t=MS),
+                in_=raw_plane[label][:].rearrange("p (j t) -> p j t", t=MS),
             )
             return codes, plane
 
-        def load_frames(r):
-            by_frame = loads.tile([P, BLOCKS, P], BF16)
-            nc.sync.dma_start(out=by_frame[:], in_=frames_by_round[r])
-            x_by_frame[r] = by_frame
-
-        def quantise(grouped, label):
-            codes = work.tile([P, WINDOWS], U32, name=label + "_codes", align_bytes=64)
-            scales = work.tile([P, WINDOWS], U8, name=label + "_scales", align_bytes=64)
-            nc.vector.quantize_mx(out=codes[:].bitcast(FP8X4), scales=scales[:], in_=grouped[:])
+        def quantise(grouped, r, label):
+            n = columns(r)
+            codes = work.tile([P, D], U32, name=label + "_codes", align_bytes=64, bufs=4)
+            scales = work.tile([P, D], U8, name=label + "_scales", align_bytes=64, bufs=4)
+            nc.vector.quantize_mx(
+                out=codes[:, :n].bitcast(FP8X4), scales=scales[:, :n], in_=grouped[:, : n * MS]
+            )
             return codes, scales
-
-        def quantise_flat(r):
-            flat_mx[r] = quantise(flat_grouped[r], "flat")
-
-        def quantise_hidden(r):
-            hidden_mx[r] = quantise(hidden_grouped[r], "hidden")
 
         def turn_frames(r, bank):
             turned = psum.tile([P, BANK_BF16], BF16, name="frames_turned", tag="bank")
@@ -113,9 +117,7 @@ def tile_dwamformer_pa_t_kernel(tc, x, w1_words, w1_scales, w2_words, w2_scales,
 
         def copy_frames(r, bank):
             if bank == 0:
-                fresh = work.tile(
-                    [P, WINDOWS * MS], BF16, name="flat_grouped", align_bytes=64, bufs=8
-                )
+                fresh = work.tile([P, D * MS], BF16, name="flat_grouped", align_bytes=64, bufs=9)
                 flat_grouped[r] = fresh
             nc.vector.tensor_copy(
                 out=flat_grouped[r][:, bank * BANK_BF16 : (bank + 1) * BANK_BF16],
@@ -124,13 +126,14 @@ def tile_dwamformer_pa_t_kernel(tc, x, w1_words, w1_scales, w2_words, w2_scales,
 
         def first_matmul(r, tile):
             codes, scales = flat_mx[r]
+            w_codes, w_plane = weight["w1"]
             cols = slice(tile * P, (tile + 1) * P)
             acc = psum.tile([P, MS, P], F32, name="hidden_acc", tag="bank")
             for t in range(MS):
                 nc.tensor.matmul_mx(
                     out=acc[:, t, :],
-                    lhsT=w1_codes[:, t * P : (t + 1) * P].bitcast(FP8X4),
-                    lhsT_scale=w1_plane[:, t * P : (t + 1) * P],
+                    lhsT=w_codes[:, t * P : (t + 1) * P].bitcast(FP8X4),
+                    lhsT_scale=w_plane[:, t * P : (t + 1) * P],
                     rhs=codes[:, cols].bitcast(FP8X4),
                     rhs_scale=scales[:, cols],
                     start=True,
@@ -138,107 +141,77 @@ def tile_dwamformer_pa_t_kernel(tc, x, w1_words, w1_scales, w2_words, w2_scales,
                 )
             hidden_acc[r, tile] = acc
 
-        def relu(r, tile, step):
+        def relu(r, tile, on_scalar):
             if tile == 0:
-                fresh = work.tile([P, WINDOWS * MS], BF16, name="hidden_grouped", align_bytes=64)
+                fresh = work.tile([P, D * MS], BF16, name="hidden_grouped", align_bytes=64)
                 hidden_grouped[r] = fresh
             dst = hidden_grouped[r][:, tile * D : (tile + 1) * D].rearrange(
                 "p (w t) -> p w t", t=MS
             )
             src = hidden_acc[r, tile][:].rearrange("p t w -> p w t")
-            if tile % 2 == 0 and not scalar_divides(step):
+            if on_scalar:
                 nc.scalar.activation(out=dst, in_=src, func=ACT.Relu)
             else:
                 nc.vector.tensor_scalar_max(out=dst, in0=src, scalar1=0.0)
 
         def second_matmul(r, m):
+            n = columns(r)
             codes, scales = hidden_mx[r]
-            acc = psum.tile([P, WINDOWS], F32, name="gate_acc", tag="bank")
+            w_codes, w_plane = weight["w2"]
+            acc = psum.tile([P, D], F32, name="gate_acc", tag="bank")
             nc.tensor.matmul_mx(
-                out=acc[:],
-                lhsT=w2_codes[:, m * P : (m + 1) * P].bitcast(FP8X4),
-                lhsT_scale=w2_plane[:, m * P : (m + 1) * P],
-                rhs=codes[:].bitcast(FP8X4),
-                rhs_scale=scales[:],
+                out=acc[:, :n],
+                lhsT=w_codes[:, m * P : (m + 1) * P].bitcast(FP8X4),
+                lhsT_scale=w_plane[:, m * P : (m + 1) * P],
+                rhs=codes[:, :n].bitcast(FP8X4),
+                rhs_scale=scales[:, :n],
                 start=True,
                 stop=True,
             )
             gate_acc[r, m] = acc
 
         def tanh(r, m):
+            n = columns(r)
             if m == 0:
-                fresh = work.tile([P, MS, WINDOWS], F32, name="weights", bufs=4)
+                fresh = work.tile([P, MS, D], F32, name="weights", bufs=4)
                 weights[r] = fresh
             nc.scalar.activation(
-                out=weights[r][:, m, :], in_=gate_acc[r, m][:], func=ACT.Tanh, scale=0.5
+                out=weights[r][:, m, :n], in_=gate_acc[r, m][:, :n], func=ACT.Tanh, scale=0.5
             )
 
         def pair(half):
             return slice(2 * half, 2 * half + 2)
 
         def exponentials(r, half):
-            part = weights[r][:, pair(half)]
+            part = weights[r][:, pair(half), : columns(r)]
             nc.scalar.activation(out=part, in_=part, func=ACT.Exp, scale=0.5)
 
         def products(r, half):
+            n = columns(r)
             if r not in weighted:
-                fresh = work.tile([P, MS, WINDOWS], F32, name="weighted")
+                fresh = work.tile([P, MS, D], F32, name="weighted")
                 weighted[r] = fresh
-            by_frame = flat_grouped[r][:].rearrange("c (w m) -> c m w", m=MS)
+            by_frame = flat_grouped[r][:, : n * MS].rearrange("c (w m) -> c m w", m=MS)
             if half == 0:
                 nc.vector.tensor_tensor(
-                    out=weighted[r][:, pair(half)],
-                    in0=weights[r][:, pair(half)],
+                    out=weighted[r][:, pair(half), :n],
+                    in0=weights[r][:, pair(half), :n],
                     in1=by_frame[:, pair(half)],
                     op=ALU.mult,
                 )
             else:
                 for m in range(2 * half, 2 * half + 2):
                     nc.gpsimd.tensor_tensor(
-                        out=weighted[r][:, m, :],
-                        in0=weights[r][:, m, :],
+                        out=weighted[r][:, m, :n],
+                        in0=weights[r][:, m, :n],
                         in1=by_frame[:, m, :],
                         op=ALU.mult,
                     )
 
-        def live(r):
-            return 0 <= r < ROUNDS
-
-        def rounds_of(n):
-            first = sum(DIVISIONS[:n])
-            return list(range(first, first + DIVISIONS[n]))
-
-        def division_of(r):
-            return [n for n in range(len(DIVISIONS)) if r in rounds_of(n)][0]
-
-        def divided_by_scalar(r):
-            return r < sum(DIVISIONS)
-
-        def place_of(r):
-            return r - rounds_of(division_of(r))[0]
-
-        def step_of_logarithms(n):
-            return rounds_of(n)[-1] + LN_AFTER
-
-        def step_of_inverse(r):
-            n = division_of(r)
-            if n == len(DIVISIONS) - 1:
-                return step_of_logarithms(n)
-            return step_of_logarithms(n) + 1 + place_of(r) // DIVIDED_IN_A_STEP
-
-        def scalar_divides(step):
-            after_logarithms = any(
-                step in (step_of_logarithms(n), step_of_logarithms(n) + 1)
-                for n in range(len(DIVISIONS))
-            )
-            return after_logarithms or any(
-                step == step_of_inverse(r) for r in range(sum(DIVISIONS))
-            )
-
         def turn_and_add(r, kind):
             terms = weighted[r] if kind == 1 else weights[r]
-            acc = psum.tile([P, TILES, P], F32, name="frames_added", tag="bank")
-            for tile in range(TILES):
+            acc = psum.tile([P, MS, P], F32, name="frames_added", tag="bank")
+            for tile in range(ROUND_TILES[r]):
                 for m in range(MS):
                     nc.tensor.matmul(
                         out=acc[:, tile, :],
@@ -250,86 +223,132 @@ def tile_dwamformer_pa_t_kernel(tc, x, w1_words, w1_scales, w2_words, w2_scales,
                     )
             frames_added[r, kind] = acc
 
-        def store(r, pooled):
-            nc.sync.dma_start(
-                out=out_by_round[r], in_=pooled[:].rearrange("w (t c) -> w t c", t=TILES)
-            )
+        def group_of(r):
+            return [g for g in range(len(GROUPS)) if r in GROUPS[g]][0]
+
+        def kept(r, kind):
+            g = group_of(r)
+            first = sum(ROUND_TILES[q] for q in GROUPS[g] if q < r)
+            return totals[g][:, kind, first : first + ROUND_TILES[r], :]
 
         def keep_sum(r, kind):
-            src = frames_added[r, kind][:].rearrange("w t c -> w (t c)")
-            if not divided_by_scalar(r):
-                if kind == 0:
-                    fresh = norm.tile([P, WINDOWS], F32, name="inverse")
-                    nc.vector.reciprocal(out=fresh[:], in_=src)
-                    inverse[r] = fresh
-                else:
-                    pooled = norm.tile([P, WINDOWS], F32, name="pooled", bufs=6)
-                    nc.vector.tensor_tensor(out=pooled[:], in0=src, in1=inverse[r][:], op=ALU.mult)
-                    store(r, pooled)
-                return
-            n = division_of(r)
-            if kind == 0 and place_of(r) == 0:
-                fresh = const.tile([P, 2, DIVISIONS[n], WINDOWS], F32, name="totals_%d" % n)
-                totals[n] = fresh
-            dst = totals[n][:, kind, place_of(r), :]
-            nc.vector.tensor_copy(out=dst, in_=src)
+            g = group_of(r)
+            if g not in totals:
+                tiles = sum(ROUND_TILES[q] for q in GROUPS[g])
+                fresh = const.tile([P, 2, tiles, P], F32, name="totals_%d" % g)
+                totals[g] = fresh
+            src = frames_added[r, kind][:, : ROUND_TILES[r], :]
+            if kind == 0:
+                nc.scalar.activation(out=kept(r, 0), in_=src, func=ACT.Square)
+            else:
+                nc.vector.tensor_copy(out=kept(r, 1), in_=src)
 
-        def logarithms(step):
-            for n in range(len(DIVISIONS)):
-                if step == step_of_logarithms(n):
-                    sums = totals[n][:, 0]
-                    nc.scalar.activation(out=sums, in_=sums, func=ACT.Ln)
+        def invert(first, last):
+            g = group_of(first)
+            start = sum(ROUND_TILES[q] for q in GROUPS[g] if q < first)
+            part = totals[g][:, 0, start : start + sum(ROUND_TILES[first : last + 1]), :]
+            nc.scalar.activation(out=part, in_=part, func=ACT.Abs_reciprocal_sqrt)
 
-        def inverses(step):
-            for r in range(sum(DIVISIONS)):
-                if step == step_of_inverse(r):
-                    log_of_sum = totals[division_of(r)][:, 0, place_of(r), :]
-                    nc.scalar.activation(out=log_of_sum, in_=log_of_sum, func=ACT.Exp, scale=-1.0)
+        def divide_and_store(r, straight=False):
+            src = frames_added[r, 1][:, : ROUND_TILES[r], :] if straight else kept(r, 1)
+            pooled = work.tile([P, MS, P], F32, name="pooled", bufs=6)
+            nc.vector.tensor_tensor(
+                out=pooled[:, : ROUND_TILES[r], :], in0=src, in1=kept(r, 0), op=ALU.mult
+            )
+            nc.sync.dma_start(
+                out=windows[:, first_tile(r) : first_tile(r) + ROUND_TILES[r], :],
+                in_=pooled[:, : ROUND_TILES[r], :],
+            )
 
-        def divide_and_store(step):
-            for r in range(sum(DIVISIONS)):
-                if step == step_of_inverse(r) + 1:
-                    both = totals[division_of(r)]
-                    pooled = norm.tile([P, WINDOWS], F32, name="pooled", bufs=6)
-                    nc.vector.tensor_tensor(
-                        out=pooled[:],
-                        in0=both[:, 1, place_of(r), :],
-                        in1=both[:, 0, place_of(r), :],
-                        op=ALU.mult,
-                    )
-                    store(r, pooled)
-
-        identity_bf16 = const.tile([P, P], BF16)
+        raw_plane = {}
+        for label in ("w1", "w2"):
+            fresh = const.tile([P, D], U8, name=label + "_raw_plane")
+            nc.vector.memset(fresh[:].bitcast(I32), 0)
+            raw_plane[label] = fresh
+        identity_bf16 = const.tile([P, P], BF16, name="identity_bf16")
         make_identity(nc, identity_bf16[:])
-        identity_f32 = const.tile([P, P], F32)
+        identity_f32 = const.tile([P, P], F32, name="identity_f32")
         make_identity(nc, identity_f32[:])
 
         load_frames(0)
-        w1_codes, w1_plane = load_weight(w1_words, w1_scales, "w1")
+        raw_w1 = load_weight(w1_words, w1_scales, "w1")
         load_frames(1)
-        w2_codes, w2_plane = load_weight(w2_words, w2_scales, "w2")
-
-        step_text = [(load_frames, -2, ()), (products, 3, (1,)), (keep_sum, 5, (1,))]
-        step_text += [(turn_frames, 0, (bank,)) for bank in range(FRAME_BANKS)]
-        step_text += [(copy_frames, 0, (bank,)) for bank in range(FRAME_BANKS)]
-        for tile in range(TILES):
-            step_text += [(first_matmul, 1, (tile,)), (relu, 1, (tile,))]
-        for m in range(MS):
-            step_text += [(second_matmul, 2, (m,)), (tanh, 2, (m,))]
-        step_text += [(exponentials, 2, (0,)), (exponentials, 2, (1,))]
-        step_text += [(logarithms, None, ()), (inverses, None, ())]
-        step_text += [(turn_and_add, 3, (0,)), (products, 3, (0,)), (divide_and_store, None, ())]
-        step_text += [(quantise_flat, 0, ()), (keep_sum, 3, (0,)), (quantise_hidden, 1, ())]
-        step_text += [(turn_and_add, 4, (1,))]
-        needs_step = (relu,)
+        raw_w2 = load_weight(w2_words, w2_scales, "w2")
+        weight = {}
 
         stack.enter_context(tc.manual_schedule())
-        for step in range(ROUNDS + 6):
-            for stage, steps_after, arguments in step_text:
-                if steps_after is None:
-                    stage(step)
-                elif live(step - steps_after):
-                    if stage in needs_step:
-                        stage(step - steps_after, *arguments, step)
+
+        gate = {}
+        ready_to_divide = []
+        inverted = 0
+        next_gate = 0
+        step = 0
+        while next_gate < ROUNDS or gate.get(step - 2) is not None or gate.get(step - 1) is not None or ready_to_divide:
+            def before(n):
+                return gate.get(step - n)
+            turning = step if step < ROUNDS else None
+            hiding = step - 1 if 0 <= step - 1 < ROUNDS else None
+            squared = before(2)
+            burst = squared is not None and squared == GROUPS[inverted][-1]
+            gating = None
+            if next_gate <= step - 2 and next_gate < ROUNDS and not (burst and inverted < len(GROUPS) - 1):
+                gating = next_gate
+                next_gate += 1
+            gate[step] = gating
+            if step + 2 < ROUNDS:
+                load_frames(step + 2)
+            if before(1) is not None:
+                products(before(1), 1)
+            tail = next_gate == ROUNDS and gating is None
+            if squared is not None:
+                keep_sum(squared, 0)
+                if squared == ROUNDS - 2:
+                    invert(GROUPS[-1][0], squared)
+                    ready_to_divide.extend(GROUPS[-1][:-1])
+                if burst:
+                    if inverted == len(GROUPS) - 1:
+                        invert(squared, squared)
                     else:
-                        stage(step - steps_after, *arguments)
+                        invert(GROUPS[inverted][0], squared)
+                        ready_to_divide.extend(GROUPS[inverted])
+            if before(3) is not None:
+                keep_sum(before(3), 1)
+            if turning is not None:
+                banks = ROUND_TILES[turning] // TILES_IN_BANK
+                for bank in range(banks):
+                    turn_frames(turning, bank)
+                for bank in range(banks):
+                    copy_frames(turning, bank)
+            if step == 0:
+                weight["w1"] = regroup_weight(raw_w1, "w1")
+            if hiding is not None:
+                for tile in range(ROUND_TILES[hiding]):
+                    first_matmul(hiding, tile)
+                    relu(hiding, tile, tile == 0 and not burst)
+            if step == 1:
+                weight["w2"] = regroup_weight(raw_w2, "w2")
+            if gating is not None:
+                for m in range(MS):
+                    second_matmul(gating, m)
+                    tanh(gating, m)
+                for half in range(2):
+                    exponentials(gating, half)
+            if before(1) is not None:
+                turn_and_add(before(1), 0)
+                products(before(1), 0)
+            if not burst or inverted == len(GROUPS) - 1:
+                for r in ready_to_divide[: (1 if next_gate < ROUNDS else 4)]:
+                    divide_and_store(r)
+                    ready_to_divide.remove(r)
+            if turning is not None:
+                flat_mx[turning] = quantise(flat_grouped[turning], turning, "flat")
+            if hiding is not None:
+                hidden_mx[hiding] = quantise(hidden_grouped[hiding], hiding, "hidden")
+            if before(2) is not None:
+                turn_and_add(before(2), 1)
+            if burst:
+                inverted += 1
+                if inverted == len(GROUPS):
+                    divide_and_store(ROUNDS - 1, True)
+                    break
+            step += 1

@@ -90,9 +90,9 @@ def tile_dwamformer_pa_t_kernel(tc, x, w1_words, w1_scales, w2_words, w2_scales,
                 in_=raw_codes[:].bitcast(I32).rearrange("p (j t) -> p t j", t=MS),
             )
             plane = const.tile([P, D], U8, name=label + "_plane", align_bytes=64)
-            nc.vector.tensor_copy(
-                out=plane[:].rearrange("p (t j) -> p j t", t=MS),
-                in_=raw_plane[label][:].rearrange("p (j t) -> p j t", t=MS),
+            nc.gpsimd.tensor_copy(
+                out=plane[:].rearrange("p (t j) -> p t j", t=MS),
+                in_=raw_plane[label][:].rearrange("p (j t) -> p t j", t=MS),
             )
             return codes, plane
 
@@ -303,7 +303,8 @@ def tile_dwamformer_pa_t_kernel(tc, x, w1_words, w1_scales, w2_words, w2_scales,
             if squared is not None:
                 keep_sum(squared, 0)
                 if squared == ROUNDS - 2:
-                    invert(GROUPS[-1][0], squared)
+                    invert(GROUPS[-1][0], squared - 3)
+                    invert(squared - 2, squared)
                     ready_to_divide.extend(GROUPS[-1][:-1])
                 if burst:
                     if inverted == len(GROUPS) - 1:
@@ -326,6 +327,7 @@ def tile_dwamformer_pa_t_kernel(tc, x, w1_words, w1_scales, w2_words, w2_scales,
                     first_matmul(hiding, tile)
                     relu(hiding, tile, tile == 0 and not burst)
             if step == 1:
+                hidden_mx[hiding] = quantise(hidden_grouped[hiding], hiding, "hidden")
                 weight["w2"] = regroup_weight(raw_w2, "w2")
             if gating is not None:
                 for m in range(MS):
@@ -336,14 +338,14 @@ def tile_dwamformer_pa_t_kernel(tc, x, w1_words, w1_scales, w2_words, w2_scales,
             if before(1) is not None:
                 turn_and_add(before(1), 0)
                 products(before(1), 0)
-            if not burst or inverted == len(GROUPS) - 1:
-                for r in ready_to_divide[: (1 if next_gate < ROUNDS else 4)]:
-                    divide_and_store(r)
-                    ready_to_divide.remove(r)
             if turning is not None:
                 flat_mx[turning] = quantise(flat_grouped[turning], turning, "flat")
-            if hiding is not None:
+            if hiding is not None and step > 1:
                 hidden_mx[hiding] = quantise(hidden_grouped[hiding], hiding, "hidden")
+            if not burst or inverted == len(GROUPS) - 1:
+                for r in ready_to_divide[: (2 if next_gate < ROUNDS else 4)]:
+                    divide_and_store(r)
+                    ready_to_divide.remove(r)
             if before(2) is not None:
                 turn_and_add(before(2), 1)
             if burst:

@@ -23,6 +23,13 @@ TILES_IN_BANK = BLOCKS_IN_BANK // MS
 ROUND_TILES = (2,) + (4,) * 15 + (2,)
 ROUNDS = len(ROUND_TILES)
 GROUPS = ((0, 1, 2, 3, 4, 5, 6, 7, 8, 9), (10, 11, 12, 13, 14, 15, 16))
+SQUARE_LAG = 2
+ADD_LAG = 1
+PAIRED = ()
+SCALAR_TILES = (0, 2)
+LATE_SCALAR_TILES = (0,)
+GPSIMD_FROM = 4
+SPLIT_TAIL = False
 
 FLOPS = 2 * 2 * WINDOWS_IN_ALL * D * D
 
@@ -54,6 +61,7 @@ def tile_dwamformer_pa_t_kernel(tc, x, w1_words, w1_scales, w2_words, w2_scales,
         gate_acc = {}
         weights = {}
         weighted = {}
+        pairs = {}
         frames_added = {}
         totals = {}
 
@@ -187,6 +195,7 @@ def tile_dwamformer_pa_t_kernel(tc, x, w1_words, w1_scales, w2_words, w2_scales,
             nc.scalar.activation(out=part, in_=part, func=ACT.Exp, scale=0.5)
 
         def products(r, half):
+            split = GPSIMD_FROM
             n = columns(r)
             if r not in weighted:
                 fresh = work.tile([P, MS, D], F32, name="weighted")
@@ -194,13 +203,13 @@ def tile_dwamformer_pa_t_kernel(tc, x, w1_words, w1_scales, w2_words, w2_scales,
             by_frame = flat_grouped[r][:, : n * MS].rearrange("c (w m) -> c m w", m=MS)
             if half == 0:
                 nc.vector.tensor_tensor(
-                    out=weighted[r][:, pair(half), :n],
-                    in0=weights[r][:, pair(half), :n],
-                    in1=by_frame[:, pair(half)],
+                    out=weighted[r][:, :split, :n],
+                    in0=weights[r][:, :split, :n],
+                    in1=by_frame[:, :split],
                     op=ALU.mult,
                 )
             else:
-                for m in range(2 * half, 2 * half + 2):
+                for m in range(split, MS):
                     nc.gpsimd.tensor_tensor(
                         out=weighted[r][:, m, :n],
                         in0=weights[r][:, m, :n],
@@ -208,18 +217,34 @@ def tile_dwamformer_pa_t_kernel(tc, x, w1_words, w1_scales, w2_words, w2_scales,
                         op=ALU.mult,
                     )
 
+        def add_pairs(r):
+            n = columns(r)
+            fresh = work.tile([P, 2, D], F32, name="pairs")
+            nc.vector.tensor_tensor(
+                out=fresh[:, :, :n],
+                in0=weights[r][:, pair(0), :n],
+                in1=weights[r][:, pair(1), :n],
+                op=ALU.add,
+            )
+            pairs[r] = fresh
+
         def turn_and_add(r, kind):
-            terms = weighted[r] if kind == 1 else weights[r]
+            if kind == 1:
+                terms, count = weighted[r], MS
+            elif r in pairs:
+                terms, count = pairs[r], 2
+            else:
+                terms, count = weights[r], MS
             acc = psum.tile([P, MS, P], F32, name="frames_added", tag="bank")
             for tile in range(ROUND_TILES[r]):
-                for m in range(MS):
+                for m in range(count):
                     nc.tensor.matmul(
                         out=acc[:, tile, :],
                         lhsT=terms[:, m, tile * P : (tile + 1) * P],
                         rhs=identity_f32[:],
                         is_transpose=True,
                         start=(m == 0),
-                        stop=(m == MS - 1),
+                        stop=(m == count - 1),
                     )
             frames_added[r, kind] = acc
 
@@ -278,42 +303,48 @@ def tile_dwamformer_pa_t_kernel(tc, x, w1_words, w1_scales, w2_words, w2_scales,
 
         stack.enter_context(tc.manual_schedule())
 
-        gate = {}
+        gate_step = {}
         ready_to_divide = []
         inverted = 0
-        next_gate = 0
         step = 0
-        while next_gate < ROUNDS or gate.get(step - 2) is not None or gate.get(step - 1) is not None or ready_to_divide:
-            def before(n):
-                return gate.get(step - n)
+        last = ROUNDS - 1
+        while inverted < len(GROUPS):
+            def at(stage_round, lag):
+                return stage_round in gate_step and gate_step[stage_round] + lag == step
+            def found(lag):
+                return [r for r in range(ROUNDS) if at(r, lag)]
+            next_gate = len(gate_step)
+            squaring = [r for r in range(ROUNDS) if at(r, 2 if r == last else SQUARE_LAG)]
+            burst = GROUPS[inverted][-1] in squaring
+            final = inverted == len(GROUPS) - 1
             turning = step if step < ROUNDS else None
             hiding = step - 1 if 0 <= step - 1 < ROUNDS else None
-            squared = before(2)
-            burst = squared is not None and squared == GROUPS[inverted][-1]
             gating = None
-            if next_gate <= step - 2 and next_gate < ROUNDS and not (burst and inverted < len(GROUPS) - 1):
+            if next_gate < ROUNDS and next_gate <= step - 2 and not burst:
                 gating = next_gate
-                next_gate += 1
-            gate[step] = gating
+                gate_step[gating] = step
             if step + 2 < ROUNDS:
                 load_frames(step + 2)
-            if before(1) is not None:
-                products(before(1), 1)
-            tail = next_gate == ROUNDS and gating is None
-            if squared is not None:
-                keep_sum(squared, 0)
-                if squared == ROUNDS - 2:
-                    invert(GROUPS[-1][0], squared - 3)
-                    invert(squared - 2, squared)
+            for r in found(1):
+                products(r, 1)
+            for r in squaring:
+                if r == last and SPLIT_TAIL:
+                    invert(GROUPS[-1][-2], GROUPS[-1][-2])
+                keep_sum(r, 0)
+                if r == last - 1:
+                    half = len(GROUPS[-1]) // 2
+                    invert(GROUPS[-1][0], GROUPS[-1][half - 1])
+                    invert(GROUPS[-1][half], last - 1)
                     ready_to_divide.extend(GROUPS[-1][:-1])
-                if burst:
-                    if inverted == len(GROUPS) - 1:
-                        invert(squared, squared)
+                if r == GROUPS[inverted][-1]:
+                    if final:
+                        invert(r, r)
                     else:
-                        invert(GROUPS[inverted][0], squared)
+                        invert(GROUPS[inverted][0], r)
                         ready_to_divide.extend(GROUPS[inverted])
-            if before(3) is not None:
-                keep_sum(before(3), 1)
+            for r in found(3):
+                if r != last:
+                    keep_sum(r, 1)
             if turning is not None:
                 banks = ROUND_TILES[turning] // TILES_IN_BANK
                 for bank in range(banks):
@@ -325,7 +356,7 @@ def tile_dwamformer_pa_t_kernel(tc, x, w1_words, w1_scales, w2_words, w2_scales,
             if hiding is not None:
                 for tile in range(ROUND_TILES[hiding]):
                     first_matmul(hiding, tile)
-                    relu(hiding, tile, tile == 0 and not burst)
+                    relu(hiding, tile, not burst and tile in (SCALAR_TILES if inverted == 0 else LATE_SCALAR_TILES))
             if step == 1:
                 hidden_mx[hiding] = quantise(hidden_grouped[hiding], hiding, "hidden")
                 weight["w2"] = regroup_weight(raw_w2, "w2")
@@ -335,22 +366,26 @@ def tile_dwamformer_pa_t_kernel(tc, x, w1_words, w1_scales, w2_words, w2_scales,
                     tanh(gating, m)
                 for half in range(2):
                     exponentials(gating, half)
-            if before(1) is not None:
-                turn_and_add(before(1), 0)
-                products(before(1), 0)
+            for r in range(ROUNDS):
+                if at(r, 1 if r == last else ADD_LAG):
+                    turn_and_add(r, 0)
+            for r in found(1):
+                products(r, 0)
+                if r in PAIRED:
+                    add_pairs(r)
             if turning is not None:
                 flat_mx[turning] = quantise(flat_grouped[turning], turning, "flat")
             if hiding is not None and step > 1:
                 hidden_mx[hiding] = quantise(hidden_grouped[hiding], hiding, "hidden")
-            if not burst or inverted == len(GROUPS) - 1:
+            if not burst or final:
                 for r in ready_to_divide[: (2 if next_gate < ROUNDS else 4)]:
                     divide_and_store(r)
                     ready_to_divide.remove(r)
-            if before(2) is not None:
-                turn_and_add(before(2), 1)
+            for r in found(2):
+                turn_and_add(r, 1)
             if burst:
                 inverted += 1
-                if inverted == len(GROUPS):
-                    divide_and_store(ROUNDS - 1, True)
-                    break
             step += 1
+        for r in ready_to_divide:
+            divide_and_store(r)
+        divide_and_store(last, True)

@@ -24,8 +24,6 @@ ROUND_TILES = (2,) + (4,) * 15 + (2,)
 ROUNDS = len(ROUND_TILES)
 GROUPS = ((0, 1, 2, 3, 4, 5, 6, 7, 8, 9), (10, 11, 12, 13, 14, 15, 16))
 SQUARE_LAG = 2
-ADD_LAG = 1
-PAIRED = ()
 SCALAR_TILES = (0, 2)
 LATE_SCALAR_TILES = (0,)
 GPSIMD_FROM = 4
@@ -220,33 +218,32 @@ def tile_dwamformer_pa_t_kernel(tc, x, w1_words, w1_scales, w2_words, w2_scales,
         def add_pairs(r):
             n = columns(r)
             fresh = work.tile([P, 2, D], F32, name="pairs")
-            nc.vector.tensor_tensor(
-                out=fresh[:, :, :n],
-                in0=weights[r][:, pair(0), :n],
-                in1=weights[r][:, pair(1), :n],
-                op=ALU.add,
-            )
+            for m in range(2):
+                nc.gpsimd.tensor_tensor(
+                    out=fresh[:, m, :n],
+                    in0=weights[r][:, m, :n],
+                    in1=weights[r][:, m + 2, :n],
+                    op=ALU.add,
+                )
             pairs[r] = fresh
 
-        def turn_and_add(r, kind):
-            if kind == 1:
-                terms, count = weighted[r], MS
-            elif r in pairs:
-                terms, count = pairs[r], 2
-            else:
-                terms, count = weights[r], MS
-            acc = psum.tile([P, MS, P], F32, name="frames_added", tag="bank")
-            for tile in range(ROUND_TILES[r]):
-                for m in range(count):
-                    nc.tensor.matmul(
-                        out=acc[:, tile, :],
-                        lhsT=terms[:, m, tile * P : (tile + 1) * P],
-                        rhs=identity_f32[:],
-                        is_transpose=True,
-                        start=(m == 0),
-                        stop=(m == count - 1),
-                    )
-            frames_added[r, kind] = acc
+        def turn_and_add(sums):
+            for r, kind in sums:
+                fresh = psum.tile([P, MS, P], F32, name="frames_added", tag="bank")
+                frames_added[r, kind] = fresh
+            for tile in range(MS):
+                for m in range(MS):
+                    for r, kind in sums:
+                        if tile < ROUND_TILES[r]:
+                            terms = weighted[r] if kind == 1 else weights[r]
+                            nc.tensor.matmul(
+                                out=frames_added[r, kind][:, tile, :],
+                                lhsT=terms[:, m, tile * P : (tile + 1) * P],
+                                rhs=identity_f32[:],
+                                is_transpose=True,
+                                start=(m == 0),
+                                stop=(m == MS - 1),
+                            )
 
         def group_of(r):
             return [g for g in range(len(GROUPS)) if r in GROUPS[g]][0]
@@ -366,13 +363,8 @@ def tile_dwamformer_pa_t_kernel(tc, x, w1_words, w1_scales, w2_words, w2_scales,
                     tanh(gating, m)
                 for half in range(2):
                     exponentials(gating, half)
-            for r in range(ROUNDS):
-                if at(r, 1 if r == last else ADD_LAG):
-                    turn_and_add(r, 0)
             for r in found(1):
                 products(r, 0)
-                if r in PAIRED:
-                    add_pairs(r)
             if turning is not None:
                 flat_mx[turning] = quantise(flat_grouped[turning], turning, "flat")
             if hiding is not None and step > 1:
@@ -381,8 +373,7 @@ def tile_dwamformer_pa_t_kernel(tc, x, w1_words, w1_scales, w2_words, w2_scales,
                 for r in ready_to_divide[: (2 if next_gate < ROUNDS else 4)]:
                     divide_and_store(r)
                     ready_to_divide.remove(r)
-            for r in found(2):
-                turn_and_add(r, 1)
+            turn_and_add([(r, 0) for r in found(1)] + [(r, 1) for r in found(2)])
             if burst:
                 inverted += 1
             step += 1

@@ -28,6 +28,7 @@ SCALAR_TILES = (0, 2)
 LATE_SCALAR_TILES = (0,)
 GPSIMD_FROM = 4
 SPLIT_TAIL = False
+PLAIN_BLOCKS = (8, 4)
 
 FLOPS = 2 * 2 * WINDOWS_IN_ALL * D * D
 
@@ -114,11 +115,14 @@ def tile_dwamformer_pa_t_kernel(tc, x, w1_words, w1_scales, w2_words, w2_scales,
         def turn_frames(r, bank):
             turned = psum.tile([P, BANK_BF16], BF16, name="frames_turned", tag="bank")
             for b in range(BLOCKS_IN_BANK):
-                nc.tensor.transpose(
-                    turned[:, b * P : (b + 1) * P],
-                    x_by_frame[r][:, bank * BLOCKS_IN_BANK + b, :],
-                    identity_bf16[:],
-                )
+                block = x_by_frame[r][:, bank * BLOCKS_IN_BANK + b, :]
+                dst = turned[:, b * P : (b + 1) * P]
+                if b < PLAIN_BLOCKS[bank]:
+                    nc.tensor.matmul(
+                        out=dst, lhsT=block, rhs=identity_bf16[:], start=True, stop=True
+                    )
+                else:
+                    nc.tensor.transpose(dst, block, identity_bf16[:])
             frames_turned[r, bank] = turned
 
         def copy_frames(r, bank):
@@ -227,11 +231,12 @@ def tile_dwamformer_pa_t_kernel(tc, x, w1_words, w1_scales, w2_words, w2_scales,
                 )
             pairs[r] = fresh
 
-        def turn_and_add(sums):
+        def turn_and_add(sums, tiles):
             for r, kind in sums:
-                fresh = psum.tile([P, MS, P], F32, name="frames_added", tag="bank")
-                frames_added[r, kind] = fresh
-            for tile in range(MS):
+                if (r, kind) not in frames_added:
+                    fresh = psum.tile([P, MS, P], F32, name="frames_added", tag="bank")
+                    frames_added[r, kind] = fresh
+            for tile in tiles:
                 for m in range(MS):
                     for r, kind in sums:
                         if tile < ROUND_TILES[r]:
@@ -324,6 +329,12 @@ def tile_dwamformer_pa_t_kernel(tc, x, w1_words, w1_scales, w2_words, w2_scales,
                 load_frames(step + 2)
             for r in found(1):
                 products(r, 1)
+            sums = [(r, 0) for r in found(2)] + [(r, 1) for r in found(3)]
+            banks = ROUND_TILES[turning] // TILES_IN_BANK if turning is not None else 0
+            for half in range(2):
+                turn_and_add(sums, range(2 * half, 2 * half + 2))
+                if half < banks:
+                    turn_frames(turning, half)
             for r in squaring:
                 if r == last and SPLIT_TAIL:
                     invert(GROUPS[-1][-2], GROUPS[-1][-2])
@@ -339,15 +350,13 @@ def tile_dwamformer_pa_t_kernel(tc, x, w1_words, w1_scales, w2_words, w2_scales,
                     else:
                         invert(GROUPS[inverted][0], r)
                         ready_to_divide.extend(GROUPS[inverted])
+            if banks > 0:
+                copy_frames(turning, 0)
             for r in found(3):
                 if r != last:
                     keep_sum(r, 1)
-            if turning is not None:
-                banks = ROUND_TILES[turning] // TILES_IN_BANK
-                for bank in range(banks):
-                    turn_frames(turning, bank)
-                for bank in range(banks):
-                    copy_frames(turning, bank)
+            if banks > 1:
+                copy_frames(turning, 1)
             if step == 0:
                 weight["w1"] = regroup_weight(raw_w1, "w1")
             if hiding is not None:
@@ -373,10 +382,10 @@ def tile_dwamformer_pa_t_kernel(tc, x, w1_words, w1_scales, w2_words, w2_scales,
                 for r in ready_to_divide[: (2 if next_gate < ROUNDS else 4)]:
                     divide_and_store(r)
                     ready_to_divide.remove(r)
-            turn_and_add([(r, 0) for r in found(1)] + [(r, 1) for r in found(2)])
             if burst:
                 inverted += 1
             step += 1
+        turn_and_add([(last, 1)], range(MS))
         for r in ready_to_divide:
             divide_and_store(r)
         divide_and_store(last, True)

@@ -23,11 +23,9 @@ TILES_IN_BANK = BLOCKS_IN_BANK // MS
 ROUND_TILES = (2,) + (4,) * 15 + (2,)
 ROUNDS = len(ROUND_TILES)
 GROUPS = ((0, 1, 2, 3, 4, 5, 6, 7, 8, 9), (10, 11, 12, 13, 14, 15, 16))
-SQUARE_LAG = 2
 SCALAR_TILES = (0, 2)
 LATE_SCALAR_TILES = (0,)
 GPSIMD_FROM = 4
-SPLIT_TAIL = False
 PLAIN_BLOCKS = (8, 4)
 
 FLOPS = 2 * 2 * WINDOWS_IN_ALL * D * D
@@ -60,7 +58,6 @@ def tile_dwamformer_pa_t_kernel(tc, x, w1_words, w1_scales, w2_words, w2_scales,
         gate_acc = {}
         weights = {}
         weighted = {}
-        pairs = {}
         frames_added = {}
         totals = {}
 
@@ -219,18 +216,6 @@ def tile_dwamformer_pa_t_kernel(tc, x, w1_words, w1_scales, w2_words, w2_scales,
                         op=ALU.mult,
                     )
 
-        def add_pairs(r):
-            n = columns(r)
-            fresh = work.tile([P, 2, D], F32, name="pairs")
-            for m in range(2):
-                nc.gpsimd.tensor_tensor(
-                    out=fresh[:, m, :n],
-                    in0=weights[r][:, m, :n],
-                    in1=weights[r][:, m + 2, :n],
-                    op=ALU.add,
-                )
-            pairs[r] = fresh
-
         def turn_and_add(sums, tiles):
             for r, kind in sums:
                 if (r, kind) not in frames_added:
@@ -297,7 +282,7 @@ def tile_dwamformer_pa_t_kernel(tc, x, w1_words, w1_scales, w2_words, w2_scales,
         identity_f32 = const.tile([P, P], F32, name="identity_f32")
         make_identity(nc, identity_f32[:])
 
-        load_frames(0)
+        load_frames(0, 2)
         raw_w1 = load_weight(w1_words, w1_scales, "w1")
         load_frames(1)
         raw_w2 = load_weight(w2_words, w2_scales, "w2")
@@ -316,7 +301,7 @@ def tile_dwamformer_pa_t_kernel(tc, x, w1_words, w1_scales, w2_words, w2_scales,
             def found(lag):
                 return [r for r in range(ROUNDS) if at(r, lag)]
             next_gate = len(gate_step)
-            squaring = [r for r in range(ROUNDS) if at(r, 2 if r == last else SQUARE_LAG)]
+            squaring = found(2)
             burst = GROUPS[inverted][-1] in squaring
             final = inverted == len(GROUPS) - 1
             turning = step if step < ROUNDS else None
@@ -329,36 +314,37 @@ def tile_dwamformer_pa_t_kernel(tc, x, w1_words, w1_scales, w2_words, w2_scales,
                 load_frames(step + 2)
             for r in found(1):
                 products(r, 1)
-            sums = [(r, 0) for r in found(2)] + [(r, 1) for r in found(3)]
+            sums = [(r, 0) for r in found(2)]
+            sums += [(r, 1) for r in found(3)]
             banks = ROUND_TILES[turning] // TILES_IN_BANK if turning is not None else 0
             for half in range(2):
                 turn_and_add(sums, range(2 * half, 2 * half + 2))
                 if half < banks:
                     turn_frames(turning, half)
             for r in squaring:
-                if r == last and SPLIT_TAIL:
-                    invert(GROUPS[-1][-2], GROUPS[-1][-2])
-                keep_sum(r, 0)
                 if r == last - 1:
                     half = len(GROUPS[-1]) // 2
                     invert(GROUPS[-1][0], GROUPS[-1][half - 1])
-                    invert(GROUPS[-1][half], last - 1)
-                    ready_to_divide.extend(GROUPS[-1][:-1])
+                    invert(GROUPS[-1][half], last - 2)
+                    ready_to_divide.extend(GROUPS[-1][:-2])
+                keep_sum(r, 0)
                 if r == GROUPS[inverted][-1]:
                     if final:
-                        invert(r, r)
+                        invert(last - 1, last)
                     else:
                         invert(GROUPS[inverted][0], r)
                         ready_to_divide.extend(GROUPS[inverted])
             if banks > 0:
                 copy_frames(turning, 0)
             for r in found(3):
-                if r != last:
+                if r < last - 1:
                     keep_sum(r, 1)
             if banks > 1:
                 copy_frames(turning, 1)
             if step == 0:
                 weight["w1"] = regroup_weight(raw_w1, "w1")
+            if step == 1:
+                flat_mx[turning] = quantise(flat_grouped[turning], turning, "flat")
             if hiding is not None:
                 for tile in range(ROUND_TILES[hiding]):
                     first_matmul(hiding, tile)
@@ -374,7 +360,7 @@ def tile_dwamformer_pa_t_kernel(tc, x, w1_words, w1_scales, w2_words, w2_scales,
                     exponentials(gating, half)
             for r in found(1):
                 products(r, 0)
-            if turning is not None:
+            if turning is not None and step != 1:
                 flat_mx[turning] = quantise(flat_grouped[turning], turning, "flat")
             if hiding is not None and step > 1:
                 hidden_mx[hiding] = quantise(hidden_grouped[hiding], hiding, "hidden")
@@ -388,4 +374,5 @@ def tile_dwamformer_pa_t_kernel(tc, x, w1_words, w1_scales, w2_words, w2_scales,
         turn_and_add([(last, 1)], range(MS))
         for r in ready_to_divide:
             divide_and_store(r)
-        divide_and_store(last, True)
+        for r in (last - 1, last):
+            divide_and_store(r, True)

@@ -22,10 +22,10 @@ BLOCKS_IN_BANK = BANK_BF16 // P
 TILES_IN_BANK = BLOCKS_IN_BANK // MS
 ROUND_TILES = (2,) + (4,) * 15 + (2,)
 ROUNDS = len(ROUND_TILES)
-GROUPS = ((0, 1, 2, 3, 4, 5, 6, 7, 8, 9), (10, 11, 12, 13, 14, 15, 16))
-SCALAR_TILES = (0, 2)
-LATE_SCALAR_TILES = (0,)
-GPSIMD_FROM = 4
+GROUPS = ((0, 1, 2, 3, 4, 5, 6, 7, 8, 9, 10), (11, 12, 13, 14, 15, 16))
+SCALAR_TILES = (0,)
+LATE_SCALAR_TILES = ()
+GPSIMD_FROM = 2
 PLAIN_BLOCKS = (8, 4)
 
 FLOPS = 2 * 2 * WINDOWS_IN_ALL * D * D
@@ -114,7 +114,7 @@ def tile_dwamformer_pa_t_kernel(tc, x, w1_words, w1_scales, w2_words, w2_scales,
             for b in range(BLOCKS_IN_BANK):
                 block = x_by_frame[r][:, bank * BLOCKS_IN_BANK + b, :]
                 dst = turned[:, b * P : (b + 1) * P]
-                if b < PLAIN_BLOCKS[bank]:
+                if b >= BLOCKS_IN_BANK - PLAIN_BLOCKS[bank]:
                     nc.tensor.matmul(
                         out=dst, lhsT=block, rhs=identity_bf16[:], start=True, stop=True
                     )
@@ -314,8 +314,7 @@ def tile_dwamformer_pa_t_kernel(tc, x, w1_words, w1_scales, w2_words, w2_scales,
                 load_frames(step + 2)
             for r in found(1):
                 products(r, 1)
-            sums = [(r, 0) for r in found(2)]
-            sums += [(r, 1) for r in found(3)]
+            sums = [(r, 0) for r in found(2)] + [(r, 1) for r in found(3)]
             banks = ROUND_TILES[turning] // TILES_IN_BANK if turning is not None else 0
             for half in range(2):
                 turn_and_add(sums, range(2 * half, 2 * half + 2))

@@ -17,12 +17,12 @@ MS = 4
 D = P * MS
 WINDOWS_IN_ALL = 8 * 1024
 BANK_BF16 = 1024
-PSUM_BANKS = 8
+PSUM_BANKS = 7
 BLOCKS_IN_BANK = BANK_BF16 // P
 TILES_IN_BANK = BLOCKS_IN_BANK // MS
 ROUND_TILES = (2,) + (4,) * 15 + (2,)
 ROUNDS = len(ROUND_TILES)
-GROUPS = ((0, 1, 2, 3, 4, 5, 6, 7, 8, 9, 10), (11, 12, 13, 14, 15, 16))
+GROUPS = ((0, 1, 2, 3, 4, 5, 6, 7, 8, 9), (10, 11, 12, 13, 14, 15, 16))
 SCALAR_TILES = (0,)
 LATE_SCALAR_TILES = ()
 GPSIMD_FROM = 2
@@ -219,7 +219,14 @@ def tile_dwamformer_pa_t_kernel(tc, x, w1_words, w1_scales, w2_words, w2_scales,
         def turn_and_add(sums, tiles):
             for r, kind in sums:
                 if (r, kind) not in frames_added:
-                    fresh = psum.tile([P, MS, P], F32, name="frames_added", tag="bank")
+                    own = kind == 0 and r < ROUNDS - 1
+                    fresh = psum.tile(
+                        [P, MS, P],
+                        F32,
+                        name="frames_added",
+                        tag="weights_added" if own else "bank",
+                        bufs=1 if own else PSUM_BANKS,
+                    )
                     frames_added[r, kind] = fresh
             for tile in tiles:
                 for m in range(MS):

from contextlib import ExitStack

import concourse.mybir as mybir
from concourse.masks import make_identity

BF16 = mybir.dt.bfloat16
F32 = mybir.dt.float32
I32 = mybir.dt.int32
U32 = mybir.dt.uint32
U8 = mybir.dt.uint8
FP8X4 = mybir.dt.float8_e4m3fn_x4
ACT = mybir.ActivationFunctionType
ALU = mybir.AluOpType

P = 128
MS = 4
D = P * MS
WINDOWS_IN_ALL = 8 * 1024
BANK_BF16 = 1024
PSUM_BANKS = 7
BLOCKS_IN_BANK = BANK_BF16 // P
TILES_IN_BANK = BLOCKS_IN_BANK // MS
ROUND_TILES = (2,) + (4,) * 15 + (2,)
ROUNDS = len(ROUND_TILES)
GROUPS = ((0, 1, 2, 3, 4, 5, 6, 7, 8, 9), (10, 11, 12, 13, 14, 15, 16))
SCALAR_TILES = (0,)
LATE_SCALAR_TILES = ()
GPSIMD_FROM = 2
PLAIN_BLOCKS = (8, 4)

FLOPS = 2 * 2 * WINDOWS_IN_ALL * D * D


def tile_dwamformer_pa_t_kernel(tc, x, w1_words, w1_scales, w2_words, w2_scales, out):
    nc = tc.nc
    frames = x.flatten_outer_dims().rearrange("(b p) c -> p b c", p=P)
    windows = out.flatten_outer_dims().rearrange("(t w) c -> w t c", w=P)

    def first_tile(r):
        return sum(ROUND_TILES[:r])

    def columns(r):
        return ROUND_TILES[r] * P

    with ExitStack() as stack:
        const = stack.enter_context(tc.tile_pool(name="const", bufs=1))
        loads = stack.enter_context(tc.tile_pool(name="loads", bufs=4))
        work = stack.enter_context(tc.tile_pool(name="work", bufs=3))
        psum = stack.enter_context(tc.psum_pool(name="psum", bufs=PSUM_BANKS))

        x_by_frame = {}
        frames_turned = {}
        flat_grouped = {}
        flat_mx = {}
        hidden_acc = {}
        hidden_grouped = {}
        hidden_mx = {}
        gate_acc = {}
        weights = {}
        weighted = {}
        frames_added = {}
        totals = {}

        def load_frames(r, pieces=1):
            tiles = ROUND_TILES[r]
            by_frame = loads.tile([P, MS * MS, P], BF16, name="by_frame")
            step = tiles * MS // pieces
            for first in range(0, tiles * MS, step):
                source = first_tile(r) * MS + first
                nc.sync.dma_start(
                    out=by_frame[:, first : first + step, :],
                    in_=frames[:, source : source + step, :],
                )
            x_by_frame[r] = by_frame

        def load_weight(words, scales, label):
            raw_codes = const.tile([P, D], U32, name=label + "_raw_codes")
            nc.sync.dma_start(
                out=raw_codes[:].bitcast(I32),
                in_=words.rearrange("g p n t -> (g p) (n t)").bitcast(I32),
            )
            rows = scales.rearrange("g q n -> (g q) n").bitcast(I32)
            for quadrant in range(4):
                nc.sync.dma_start(
                    out=raw_plane[label][32 * quadrant : 32 * quadrant + 4, :].bitcast(I32),
                    in_=rows[4 * quadrant : 4 * quadrant + 4, :],
                )
            return raw_codes

        def regroup_weight(raw_codes, label):
            codes = const.tile([P, D], U32, name=label + "_codes", align_bytes=64)
            nc.vector.tensor_copy(
                out=codes[:].bitcast(I32).rearrange("p (t j) -> p t j", t=MS),
                in_=raw_codes[:].bitcast(I32).rearrange("p (j t) -> p t j", t=MS),
            )
            plane = const.tile([P, D], U8, name=label + "_plane", align_bytes=64)
            nc.gpsimd.tensor_copy(
                out=plane[:].rearrange("p (t j) -> p t j", t=MS),
                in_=raw_plane[label][:].rearrange("p (j t) -> p t j", t=MS),
            )
            return codes, plane

        def quantise(grouped, r, label):
            n = columns(r)
            codes = work.tile([P, D], U32, name=label + "_codes", align_bytes=64, bufs=4)
            scales = work.tile([P, D], U8, name=label + "_scales", align_bytes=64, bufs=4)
            nc.vector.quantize_mx(
                out=codes[:, :n].bitcast(FP8X4), scales=scales[:, :n], in_=grouped[:, : n * MS]
            )
            return codes, scales

        def turn_frames(r, bank):
            turned = psum.tile([P, BANK_BF16], BF16, name="frames_turned", tag="bank")
            for b in range(BLOCKS_IN_BANK):
                block = x_by_frame[r][:, bank * BLOCKS_IN_BANK + b, :]
                dst = turned[:, b * P : (b + 1) * P]
                if b >= BLOCKS_IN_BANK - PLAIN_BLOCKS[bank]:
                    nc.tensor.matmul(
                        out=dst, lhsT=block, rhs=identity_bf16[:], start=True, stop=True
                    )
                else:
                    nc.tensor.transpose(dst, block, identity_bf16[:])
            frames_turned[r, bank] = turned

        def copy_frames(r, bank):
            if bank == 0:
                fresh = work.tile([P, D * MS], BF16, name="flat_grouped", align_bytes=64, bufs=9)
                flat_grouped[r] = fresh
            nc.vector.tensor_copy(
                out=flat_grouped[r][:, bank * BANK_BF16 : (bank + 1) * BANK_BF16],
                in_=frames_turned[r, bank][:],
            )

        def first_matmul(r, tile):
            codes, scales = flat_mx[r]
            w_codes, w_plane = weight["w1"]
            cols = slice(tile * P, (tile + 1) * P)
            acc = psum.tile([P, MS, P], F32, name="hidden_acc", tag="bank")
            for t in range(MS):
                nc.tensor.matmul_mx(
                    out=acc[:, t, :],
                    lhsT=w_codes[:, t * P : (t + 1) * P].bitcast(FP8X4),
                    lhsT_scale=w_plane[:, t * P : (t + 1) * P],
                    rhs=codes[:, cols].bitcast(FP8X4),
                    rhs_scale=scales[:, cols],
                    start=True,
                    stop=True,
                )
            hidden_acc[r, tile] = acc

        def relu(r, tile, on_scalar):
            if tile == 0:
                fresh = work.tile([P, D * MS], BF16, name="hidden_grouped", align_bytes=64)
                hidden_grouped[r] = fresh
            dst = hidden_grouped[r][:, tile * D : (tile + 1) * D].rearrange(
                "p (w t) -> p w t", t=MS
            )
            src = hidden_acc[r, tile][:].rearrange("p t w -> p w t")
            if on_scalar:
                nc.scalar.activation(out=dst, in_=src, func=ACT.Relu)
            else:
                nc.vector.tensor_scalar_max(out=dst, in0=src, scalar1=0.0)

        def second_matmul(r, m):
            n = columns(r)
            codes, scales = hidden_mx[r]
            w_codes, w_plane = weight["w2"]
            acc = psum.tile([P, D], F32, name="gate_acc", tag="bank")
            nc.tensor.matmul_mx(
                out=acc[:, :n],
                lhsT=w_codes[:, m * P : (m + 1) * P].bitcast(FP8X4),
                lhsT_scale=w_plane[:, m * P : (m + 1) * P],
                rhs=codes[:, :n].bitcast(FP8X4),
                rhs_scale=scales[:, :n],
                start=True,
                stop=True,
            )
            gate_acc[r, m] = acc

        def tanh(r, m):
            n = columns(r)
            if m == 0:
                fresh = work.tile([P, MS, D], F32, name="weights", bufs=4)
                weights[r] = fresh
            nc.scalar.activation(
                out=weights[r][:, m, :n], in_=gate_acc[r, m][:, :n], func=ACT.Tanh, scale=0.5
            )

        def pair(half):
            return slice(2 * half, 2 * half + 2)

        def exponentials(r, half):
            part = weights[r][:, pair(half), : columns(r)]
            nc.scalar.activation(out=part, in_=part, func=ACT.Exp, scale=0.5)

        def products(r, half):
            split = GPSIMD_FROM
            n = columns(r)
            if r not in weighted:
                fresh = work.tile([P, MS, D], F32, name="weighted")
                weighted[r] = fresh
            by_frame = flat_grouped[r][:, : n * MS].rearrange("c (w m) -> c m w", m=MS)
            if half == 0:
                nc.vector.tensor_tensor(
                    out=weighted[r][:, :split, :n],
                    in0=weights[r][:, :split, :n],
                    in1=by_frame[:, :split],
                    op=ALU.mult,
                )
            else:
                for m in range(split, MS):
                    nc.gpsimd.tensor_tensor(
                        out=weighted[r][:, m, :n],
                        in0=weights[r][:, m, :n],
                        in1=by_frame[:, m, :],
                        op=ALU.mult,
                    )

        def turn_and_add(sums, tiles):
            for r, kind in sums:
                if (r, kind) not in frames_added:
                    own = kind == 0 and r < ROUNDS - 1
                    fresh = psum.tile(
                        [P, MS, P],
                        F32,
                        name="frames_added",
                        tag="weights_added" if own else "bank",
                        bufs=1 if own else PSUM_BANKS,
                    )
                    frames_added[r, kind] = fresh
            for tile in tiles:
                for m in range(MS):
                    for r, kind in sums:
                        if tile < ROUND_TILES[r]:
                            terms = weighted[r] if kind == 1 else weights[r]
                            nc.tensor.matmul(
                                out=frames_added[r, kind][:, tile, :],
                                lhsT=terms[:, m, tile * P : (tile + 1) * P],
                                rhs=identity_f32[:],
                                is_transpose=True,
                                start=(m == 0),
                                stop=(m == MS - 1),
                            )

        def group_of(r):
            return [g for g in range(len(GROUPS)) if r in GROUPS[g]][0]

        def kept(r, kind):
            g = group_of(r)
            first = sum(ROUND_TILES[q] for q in GROUPS[g] if q < r)
            return totals[g][:, kind, first : first + ROUND_TILES[r], :]

        def keep_sum(r, kind):
            g = group_of(r)
            if g not in totals:
                tiles = sum(ROUND_TILES[q] for q in GROUPS[g])
                fresh = const.tile([P, 2, tiles, P], F32, name="totals_%d" % g)
                totals[g] = fresh
            src = frames_added[r, kind][:, : ROUND_TILES[r], :]
            if kind == 0:
                nc.scalar.activation(out=kept(r, 0), in_=src, func=ACT.Square)
            else:
                nc.vector.tensor_copy(out=kept(r, 1), in_=src)

        def invert(first, last):
            g = group_of(first)
            start = sum(ROUND_TILES[q] for q in GROUPS[g] if q < first)
            part = totals[g][:, 0, start : start + sum(ROUND_TILES[first : last + 1]), :]
            nc.scalar.activation(out=part, in_=part, func=ACT.Abs_reciprocal_sqrt)

        def divide_and_store(r, straight=False):
            src = frames_added[r, 1][:, : ROUND_TILES[r], :] if straight else kept(r, 1)
            pooled = work.tile([P, MS, P], F32, name="pooled", bufs=6)
            nc.vector.tensor_tensor(
                out=pooled[:, : ROUND_TILES[r], :], in0=src, in1=kept(r, 0), op=ALU.mult
            )
            nc.sync.dma_start(
                out=windows[:, first_tile(r) : first_tile(r) + ROUND_TILES[r], :],
                in_=pooled[:, : ROUND_TILES[r], :],
            )

        raw_plane = {}
        for label in ("w1", "w2"):
            fresh = const.tile([P, D], U8, name=label + "_raw_plane")
            nc.vector.memset(fresh[:].bitcast(I32), 0)
            raw_plane[label] = fresh
        identity_bf16 = const.tile([P, P], BF16, name="identity_bf16")
        make_identity(nc, identity_bf16[:])
        identity_f32 = const.tile([P, P], F32, name="identity_f32")
        make_identity(nc, identity_f32[:])

        load_frames(0, 2)
        raw_w1 = load_weight(w1_words, w1_scales, "w1")
        load_frames(1)
        raw_w2 = load_weight(w2_words, w2_scales, "w2")
        weight = {}

        stack.enter_context(tc.manual_schedule())

        gate_step = {}
        ready_to_divide = []
        inverted = 0
        step = 0
        last = ROUNDS - 1
        while inverted < len(GROUPS):
            def at(stage_round, lag):
                return stage_round in gate_step and gate_step[stage_round] + lag == step
            def found(lag):
                return [r for r in range(ROUNDS) if at(r, lag)]
            next_gate = len(gate_step)
            squaring = found(2)
            burst = GROUPS[inverted][-1] in squaring
            final = inverted == len(GROUPS) - 1
            turning = step if step < ROUNDS else None
            hiding = step - 1 if 0 <= step - 1 < ROUNDS else None
            gating = None
            if next_gate < ROUNDS and next_gate <= step - 2 and not burst:
                gating = next_gate
                gate_step[gating] = step
            if step + 2 < ROUNDS:
                load_frames(step + 2)
            for r in found(1):
                products(r, 1)
            sums = [(r, 0) for r in found(2)] + [(r, 1) for r in found(3)]
            banks = ROUND_TILES[turning] // TILES_IN_BANK if turning is not None else 0
            for half in range(2):
                turn_and_add(sums, range(2 * half, 2 * half + 2))
                if half < banks:
                    turn_frames(turning, half)
            for r in squaring:
                if r == last - 1:
                    half = len(GROUPS[-1]) // 2
                    invert(GROUPS[-1][0], GROUPS[-1][half - 1])
                    invert(GROUPS[-1][half], last - 2)
                    ready_to_divide.extend(GROUPS[-1][:-2])
                keep_sum(r, 0)
                if r == GROUPS[inverted][-1]:
                    if final:
                        invert(last - 1, last)
                    else:
                        invert(GROUPS[inverted][0], r)
                        ready_to_divide.extend(GROUPS[inverted])
            if banks > 0:
                copy_frames(turning, 0)
            for r in found(3):
                if r < last - 1:
                    keep_sum(r, 1)
            if banks > 1:
                copy_frames(turning, 1)
            if step == 0:
                weight["w1"] = regroup_weight(raw_w1, "w1")
            if step == 1:
                flat_mx[turning] = quantise(flat_grouped[turning], turning, "flat")
            if hiding is not None:
                for tile in range(ROUND_TILES[hiding]):
                    first_matmul(hiding, tile)
                    relu(hiding, tile, not burst and tile in (SCALAR_TILES if inverted == 0 else LATE_SCALAR_TILES))
            if step == 1:
                hidden_mx[hiding] = quantise(hidden_grouped[hiding], hiding, "hidden")
                weight["w2"] = regroup_weight(raw_w2, "w2")
            if gating is not None:
                for m in range(MS):
                    second_matmul(gating, m)
                    tanh(gating, m)
                for half in range(2):
                    exponentials(gating, half)
            for r in found(1):
                products(r, 0)
            if turning is not None and step != 1:
                flat_mx[turning] = quantise(flat_grouped[turning], turning, "flat")
            if hiding is not None and step > 1:
                hidden_mx[hiding] = quantise(hidden_grouped[hiding], hiding, "hidden")
            if not burst or final:
                for r in ready_to_divide[: (2 if next_gate < ROUNDS else 4)]:
                    divide_and_store(r)
                    ready_to_divide.remove(r)
            if burst:
                inverted += 1
            step += 1
        turn_and_add([(last, 1)], range(MS))
        for r in ready_to_divide:
            divide_and_store(r)
        for r in (last - 1, last):
            divide_and_store(r, True)
